import numpy as np
import ml_dtypes


def mxq(x, axis, fmt="e4m3"):
    dtype, down = {"e4m3": (ml_dtypes.float8_e4m3fn, 7), "e5m2": (ml_dtypes.float8_e5m2, 14)}[fmt]
    v = np.moveaxis(np.asarray(x, np.float32).astype(ml_dtypes.bfloat16).astype(np.float64), axis, -1)
    blocks = v.reshape(v.shape[:-1] + (-1, 32))
    amax = np.abs(blocks).max(-1, keepdims=True)
    byte = np.maximum(np.where(amax > 0, np.frexp(amax)[1] - 1 + 127, 0) - down, 1)
    scale = np.exp2(byte - 127.0)
    codes = (blocks / scale).astype(np.float32).astype(dtype).astype(np.float64)
    return np.moveaxis((codes * scale).reshape(v.shape), -1, axis)


WIDE = False


def mx_kscale(k):
    if not WIDE:
        return np.ones(k)
    levels = np.array([10, -10, 5, -5, 0])
    a = np.random.permutation(np.resize(levels, k // 512 * 4)).reshape(k // 512, 4)
    idx = np.arange(k)
    return np.exp2(a[idx // 512, idx % 128 // 32])


BF16 = ml_dtypes.bfloat16


def bf(x):
    return np.asarray(x, np.float32).astype(BF16)


def f64(x):
    return np.asarray(x).astype(np.float64)


E2M1 = np.array([0.0, 0.5, 1.0, 1.5, 2.0, 3.0, 4.0, 6.0, -0.0, -0.5, -1.0, -1.5, -2.0, -3.0, -4.0, -6.0])


def pack_weight(w, fmt):
    k, n = w.shape
    w = f64(bf(w)).reshape(k // 32, 32, n)
    amax = np.abs(w).max(1)
    if fmt == "e4m3":
        byte = np.frexp(amax)[1] - 1 + 127 - 7
    else:
        mant, ex = np.frexp(amax / 6.0)
        byte = np.where(mant > 0.5, ex, ex - 1) + 127
    byte = np.clip(np.where(amax > 0, byte, 1), 1, 254)
    scaled = (w * np.exp2(127.0 - byte)[:, None, :]).reshape(k, n).astype(np.float32)
    by_word = np.ascontiguousarray(scaled.reshape(k // 512, 128, 4, n).transpose(0, 1, 3, 2))
    if fmt == "e4m3":
        words = by_word.astype(ml_dtypes.float8_e4m3fn).view(np.uint8)
    else:
        c = by_word.astype(ml_dtypes.float4_e2m1fn).view(np.uint8) & 0xF
        words = c[..., 0::2] | (c[..., 1::2] << 4)
    return np.ascontiguousarray(words), np.ascontiguousarray(byte.astype(np.uint8).reshape(k // 512, 16, n))


def unpack_weight(words, scales, fmt):
    g, p, n, _ = words.shape
    if fmt == "e4m3":
        vals = np.ascontiguousarray(words).view(ml_dtypes.float8_e4m3fn).astype(np.float64)
    else:
        nib = np.empty((g, p, n, 4), np.uint8)
        nib[..., 0::2] = words & 0xF
        nib[..., 1::2] = words >> 4
        vals = E2M1[nib]
    vals = vals * np.repeat(np.exp2(scales.astype(np.float64) - 127.0), 8, axis=1)[..., None]
    return vals.transpose(0, 1, 3, 2).reshape(g * 512, n)

def pack4(w):
    words, scales = pack_weight(w, "e2m1")
    return words.reshape(words.shape[0], 128, -1), scales


def unpack4(words, scales):
    return unpack_weight(words.reshape(words.shape[0], 128, -1, 2), scales, "e2m1")


B, HH, WW, C, NH, DIM = 2, 8, 16, 16384, 8, 32
N = HH * WW
HD = NH * DIM
F = 4 * HD
BN_EPS = 1e-5
WS = 0.02
GQK = np.sqrt(2.8) / DIM ** 0.25
GV = 4.0


def heads(t):
    return t.reshape(B, N, NH, DIM).transpose(0, 2, 1, 3)


def setup_inputs():
    s = mx_kscale(C)
    x = np.random.standard_normal((B, HH, WW, C)) + 0.5 * np.random.standard_normal(C)
    gain = np.concatenate([np.full(2 * HD, GQK), np.full(2 * HD, GV)])
    inputs = bf(x * s)
    words, scales = pack4(np.random.standard_normal((C, F)) * WS / np.sqrt(C) / s[:, None])
    return {"inputs": inputs,
            "w_qkv_words": words,
            "w_qkv_scales": scales,
            "bn_scale": bf(np.random.standard_normal(F) * gain)}


def reference(inputs, w_qkv_words, w_qkv_scales, bn_scale):
    x = mxq(f64(inputs).reshape(B * N, C), 1, "e4m3") @ unpack4(w_qkv_words, w_qkv_scales)
    mean = x.mean(axis=0)
    var = x.var(axis=0)
    x = (x - mean) / np.sqrt(var + BN_EPS) * f64(bn_scale)
    q, k, v1, v2 = (heads(t) for t in np.split(x.reshape(B, N, F), 4, axis=-1))
    v = np.concatenate((v1, v2), axis=-1)
    return np.ascontiguousarray(q), np.ascontiguousarray(k), v

@@ -1,0 +1,271 @@
+from contextlib import ExitStack
+
+import concourse.mybir as mybir
+from concourse.masks import make_identity
+
+F32 = mybir.dt.float32
+BF16 = mybir.dt.bfloat16
+I32 = mybir.dt.int32
+U32 = mybir.dt.uint32
+U8 = mybir.dt.uint8
+FP8X4 = mybir.dt.float8_e4m3fn_x4
+FP4X4 = mybir.dt.float4_e2m1fn_x4
+ACT = mybir.ActivationFunctionType
+ALU = mybir.AluOpType
+
+P = 128
+ROW_TILES = 2
+CHANNELS = 16384
+K_PASS = 512
+PASSES = CHANNELS // K_PASS
+COLS = 1024
+HALF = 512
+HALVES = COLS // HALF
+COL_TILES = COLS // P
+TILES_PER_HALF = HALF // P
+CHUNK = 4
+CHUNKS = PASSES // CHUNK
+SCALE_GROUP = 8
+HEADS = 8
+DIM = 32
+BN_EPS = 1e-5
+
+FLOPS = 2 * ROW_TILES * P * CHANNELS * COLS
+
+
+def tile_levitattention_pa_k_kernel(tc, inputs, w_qkv_words, w_qkv_scales, bn_scale, out_0, out_1, out_2):
+    nc = tc.nc
+    x_dram = inputs.rearrange("b h w c -> (b h w) c")
+
+    with ExitStack() as ctx:
+        ctx.enter_context(tc.manual_schedule())
+        const = ctx.enter_context(tc.tile_pool(name="const", bufs=1))
+        resident = ctx.enter_context(tc.tile_pool(name="resident", bufs=1))
+        stage = ctx.enter_context(tc.tile_pool(name="stage", bufs=2))
+        tail = ctx.enter_context(tc.tile_pool(name="tail", bufs=2))
+        sums = ctx.enter_context(tc.psum_pool(name="sums", bufs=1))
+        banks = ctx.enter_context(tc.psum_pool(name="banks", bufs=4))
+
+        x_in = resident.tile([P, CHUNKS, ROW_TILES, CHUNK * K_PASS], BF16)
+        w_words = [
+            resident.tile([P, CHUNK, 2 * COLS], U8, name="w_words%d" % j, align_bytes=64) for j in range(CHUNKS)
+        ]
+        w_scales = [
+            resident.tile([P, SCALE_GROUP, COLS], U8, name="w_scales%d" % s, align_bytes=64)
+            for s in range(PASSES // SCALE_GROUP)
+        ]
+
+        def zero_scale_planes(s):
+            nc.vector.memset(w_scales[s][:].bitcast(I32), 0)
+
+        zero_scale_planes(0)
+        eps = const.tile([P, 1], F32)
+        nc.vector.memset(eps[:], BN_EPS)
+        gain_rows = const.tile([P, P], BF16)
+        nc.vector.memset(gain_rows[:], 0.0)
+        for s in range(1, PASSES // SCALE_GROUP):
+            zero_scale_planes(s)
+        ident = const.tile([P, P], F32)
+        make_identity(nc, ident[:])
+        warm = const.tile([P, 1], F32)
+        nc.scalar.activation(out=warm[:], in_=eps[:], func=ACT.Sqrt)
+        nc.scalar.dma_start(out=gain_rows[0:COL_TILES, :], in_=bn_scale.rearrange("(t c) -> t c", c=P))
+
+        def load_x(j):
+            cols = slice(j * CHUNK * K_PASS, (j + 1) * CHUNK * K_PASS)
+            nc.sync.dma_start(out=x_in[:, j], in_=x_dram[:, cols].rearrange("(rt p) k -> p rt k", p=P))
+
+        def load_w_scales(s):
+            group = slice(s * SCALE_GROUP, (s + 1) * SCALE_GROUP)
+            for b in range(2):
+                for r in range(4):
+                    nc.sync.dma_start(
+                        out=w_scales[s][32 * b + r : P : 64, :, :].bitcast(I32),
+                        in_=w_qkv_scales[group, 4 * b + r : 16 : 8, :].rearrange("g q n -> q g n").bitcast(I32),
+                    )
+
+        def load_w(j):
+            group = slice(j * CHUNK, (j + 1) * CHUNK)
+            nc.sync.dma_start(
+                out=w_words[j][:].bitcast(I32),
+                in_=w_qkv_words[group].rearrange("g p n -> p g n").bitcast(I32),
+            )
+
+        load_x(0)
+        load_x(1)
+        for j in range(CHUNKS):
+            if (j * CHUNK) % SCALE_GROUP == 0:
+                load_w_scales(j * CHUNK // SCALE_GROUP)
+            load_w(j)
+            if j + 2 < CHUNKS:
+                load_x(j + 2)
+
+        sorted_of = {}
+        codes_of = {}
+
+        def sort_words(j):
+            x_sorted = stage.tile([P, ROW_TILES, CHUNK, 2, P], F32)
+            for rt in range(ROW_TILES):
+                nc.vector.tensor_copy(
+                    out=x_sorted[:, rt],
+                    in_=x_in[:, j, rt, :].bitcast(F32).rearrange("r (g q u) -> r g u q", g=CHUNK, u=2),
+                )
+            sorted_of[j] = x_sorted
+
+        def transpose_and_quantise(j):
+            x_sorted = sorted_of[j]
+            grouped = stage.tile([P, CHUNK, ROW_TILES * P * 4], BF16, align_bytes=64)
+            x_codes = stage.tile([P, CHUNK, ROW_TILES * P], U32, align_bytes=64)
+            x_scales = stage.tile([P, CHUNK, ROW_TILES * P], U8, align_bytes=64)
+            for g in range(CHUNK):
+                bank = banks.tile([P, ROW_TILES, 2, P], F32, tag="bank")
+                for rt in range(ROW_TILES):
+                    for u in range(2):
+                        nc.tensor.transpose(out=bank[:, rt, u, :], in_=x_sorted[:, rt, g, u, :], identity=ident[:])
+                nc.scalar.copy(
+                    out=grouped[:, g, :].bitcast(F32).rearrange("q (rt r u) -> q rt r u", rt=ROW_TILES, u=2),
+                    in_=bank[:].rearrange("q rt u r -> q rt r u"),
+                )
+                nc.vector.quantize_mx(
+                    out=x_codes[:, g, :].bitcast(FP8X4),
+                    scales=x_scales[:, g, :],
+                    in_=grouped[:, g, :],
+                )
+            codes_of[j] = (x_codes, x_scales)
+
+        acc = {}
+        for rt in range(ROW_TILES):
+            for ch in range(HALVES):
+                acc[(rt, ch)] = sums.tile([P, HALF], F32, name="acc%d%d" % (rt, ch))
+
+        def multiply(j):
+            x_codes, x_scales = codes_of[j]
+            for ch in range(HALVES):
+                for g in range(CHUNK):
+                    k = j * CHUNK + g
+                    for rt in range(ROW_TILES):
+                        rows = slice(rt * P, (rt + 1) * P)
+                        nc.tensor.matmul_mx(
+                            out=acc[(rt, ch)][:],
+                            lhsT=x_codes[:, g, rows].bitcast(FP8X4),
+                            lhsT_scale=x_scales[:, g, rows],
+                            rhs=w_words[j][:, g, ch * 2 * HALF : (ch + 1) * 2 * HALF].bitcast(FP4X4),
+                            rhs_scale=w_scales[k // SCALE_GROUP][:, k % SCALE_GROUP, ch * HALF : (ch + 1) * HALF],
+                            start=(k == 0),
+                            stop=(k == PASSES - 1),
+                        )
+
+        sort_words(0)
+        transpose_and_quantise(0)
+        sort_words(1)
+        transpose_and_quantise(1)
+
+        gain_f32 = const.tile([P, P], F32)
+        nc.vector.tensor_copy(out=gain_f32[:], in_=gain_rows[:])
+        gain_bank = banks.tile([P, ROW_TILES, 2, P], F32, tag="bank")
+        nc.tensor.transpose(out=gain_bank[:, 0, 0, :], in_=gain_f32[:], identity=ident[:])
+        gain = const.tile([P, COL_TILES], F32)
+        nc.vector.tensor_copy(out=gain[:], in_=gain_bank[:, 0, 0, 0:COL_TILES])
+
+        for j in range(CHUNKS):
+            if j + 2 < CHUNKS:
+                sort_words(j + 2)
+            multiply(j)
+            if j + 2 < CHUNKS:
+                transpose_and_quantise(j + 2)
+
+        x_cols = {}
+        mean_var = {}
+        std = {}
+        y_cols = {}
+
+        def column_statistics(ch):
+            x_rows = tail.tile([P, ROW_TILES, HALF], F32)
+            for rt in range(ROW_TILES):
+                nc.scalar.copy(out=x_rows[:, rt, :], in_=acc[(rt, ch)][:])
+            stats = tail.tile([P, TILES_PER_HALF, 6], F32)
+            mean_var[ch] = tail.tile([P, TILES_PER_HALF, 2], F32, name="mean_var")
+            for pair in range(TILES_PER_HALF // 2):
+                bank = banks.tile([P, 2, ROW_TILES * P], F32, tag="bank")
+                for i in range(2):
+                    t = 2 * pair + i
+                    for rt in range(ROW_TILES):
+                        nc.tensor.transpose(
+                            out=bank[:, i, rt * P : (rt + 1) * P],
+                            in_=x_rows[:, rt, t * P : (t + 1) * P],
+                            identity=ident[:],
+                        )
+                    x_cols[(ch, t)] = bank[:, i, :]
+                    nc.vector.bn_stats(out=stats[:, t, :], in_=x_cols[(ch, t)])
+                    nc.vector.bn_aggr(out=mean_var[ch][:, t, :], in_=stats[:, t, :])
+
+        def standard_deviation(ch):
+            std[ch] = tail.tile([P, TILES_PER_HALF], F32, name="std")
+            nc.scalar.activation(out=std[ch][:], in_=mean_var[ch][:, :, 1], func=ACT.Sqrt, bias=eps[:])
+
+        def normalise(ch):
+            factor = tail.tile([P, TILES_PER_HALF], F32)
+            shift = tail.tile([P, TILES_PER_HALF], F32)
+            nc.vector.reciprocal(out=factor[:], in_=std[ch][:])
+            nc.vector.tensor_mul(
+                out=factor[:], in0=factor[:], in1=gain[:, ch * TILES_PER_HALF : (ch + 1) * TILES_PER_HALF]
+            )
+            nc.vector.scalar_tensor_tensor(
+                out=shift[:], in0=mean_var[ch][:, :, 0], scalar=-1.0, in1=factor[:], op0=ALU.mult, op1=ALU.mult
+            )
+            y_cols[ch] = tail.tile([P, TILES_PER_HALF, ROW_TILES * P], F32, name="y_cols")
+            for t in range(TILES_PER_HALF):
+                if t % 2 == 0:
+                    nc.vector.tensor_scalar(
+                        out=y_cols[ch][:, t, :],
+                        in0=x_cols[(ch, t)],
+                        scalar1=factor[:, t : t + 1],
+                        scalar2=shift[:, t : t + 1],
+                        op0=ALU.mult,
+                        op1=ALU.add,
+                    )
+                else:
+                    nc.scalar.activation(
+                        out=y_cols[ch][:, t, :],
+                        in_=x_cols[(ch, t)],
+                        func=ACT.Identity,
+                        scale=factor[:, t : t + 1],
+                        bias=shift[:, t : t + 1],
+                    )
+
+        def store(ch):
+            for rt in range(ROW_TILES):
+                y_bank = sums.tile([P, HALF], F32, tag="acc%d%d" % (rt, ch))
+                for t in range(TILES_PER_HALF):
+                    nc.tensor.transpose(
+                        out=y_bank[:, t * P : (t + 1) * P],
+                        in_=y_cols[ch][:, t, rt * P : (rt + 1) * P],
+                        identity=ident[:],
+                    )
+                y_rows = tail.tile([P, HALF], F32, bufs=ROW_TILES * HALVES)
+                copy_out = nc.scalar.copy if rt == 0 else nc.vector.tensor_copy
+                if ch == 0:
+                    copy_out(out=y_rows[:], in_=y_bank[:])
+                    for out_dram, first in ((out_0, 0), (out_1, HEADS * DIM)):
+                        nc.sync.dma_start(
+                            out=out_dram[rt].rearrange("h n d -> n h d"),
+                            in_=y_rows[:, first : first + HEADS * DIM].rearrange("n (h d) -> n h d", d=DIM),
+                        )
+                else:
+                    copy_out(
+                        out=y_rows[:].rearrange("n (h v d) -> n h v d", v=2, d=DIM),
+                        in_=y_bank[:].rearrange("n (v h d) -> n h v d", v=2, d=DIM),
+                    )
+                    nc.sync.dma_start(
+                        out=out_2[rt].rearrange("h n e -> n h e"),
+                        in_=y_rows[:].rearrange("n (h e) -> n h e", e=2 * DIM),
+                    )
+
+        for ch in range(HALVES):
+            column_statistics(ch)
+        for ch in range(HALVES):
+            standard_deviation(ch)
+        for ch in range(HALVES):
+            normalise(ch)
+        for ch in range(HALVES):
+            store(ch)

@@ -77,12 +77,11 @@ def tile_levitattention_pa_k_kernel(tc, inputs, w_qkv_words, w_qkv_scales, bn_sc
 
         def load_w_scales(s):
             group = slice(s * SCALE_GROUP, (s + 1) * SCALE_GROUP)
-            for b in range(2):
-                for r in range(4):
-                    nc.sync.dma_start(
-                        out=w_scales[s][32 * b + r : P : 64, :, :].bitcast(I32),
-                        in_=w_qkv_scales[group, 4 * b + r : 16 : 8, :].rearrange("g q n -> q g n").bitcast(I32),
-                    )
+            for r in range(4):
+                nc.gpsimd.dma_start(
+                    out=w_scales[s][r : P : 32, :, :].bitcast(F32),
+                    in_=w_qkv_scales[group, r : 16 : 4, :].rearrange("g q n -> q g n").bitcast(F32),
+                )
 
         def load_w(j):
             group = slice(j * CHUNK, (j + 1) * CHUNK)
@@ -91,11 +90,11 @@ def tile_levitattention_pa_k_kernel(tc, inputs, w_qkv_words, w_qkv_scales, bn_sc
                 in_=w_qkv_words[group].rearrange("g p n -> p g n").bitcast(I32),
             )
 
+        for s in range(PASSES // SCALE_GROUP):
+            load_w_scales(s)
         load_x(0)
         load_x(1)
         for j in range(CHUNKS):
-            if (j * CHUNK) % SCALE_GROUP == 0:
-                load_w_scales(j * CHUNK // SCALE_GROUP)
             load_w(j)
             if j + 2 < CHUNKS:
                 load_x(j + 2)

@@ -77,11 +77,12 @@ def tile_levitattention_pa_k_kernel(tc, inputs, w_qkv_words, w_qkv_scales, bn_sc
 
         def load_w_scales(s):
             group = slice(s * SCALE_GROUP, (s + 1) * SCALE_GROUP)
-            for r in range(4):
-                nc.gpsimd.dma_start(
-                    out=w_scales[s][r : P : 32, :, :].bitcast(F32),
-                    in_=w_qkv_scales[group, r : 16 : 4, :].rearrange("g q n -> q g n").bitcast(F32),
-                )
+            for b in range(2):
+                for r in range(4):
+                    nc.sync.dma_start(
+                        out=w_scales[s][32 * b + r : P : 64, :, :].bitcast(I32),
+                        in_=w_qkv_scales[group, 4 * b + r : 16 : 8, :].rearrange("g q n -> q g n").bitcast(I32),
+                    )
 
         def load_w(j):
             group = slice(j * CHUNK, (j + 1) * CHUNK)
@@ -90,11 +91,11 @@ def tile_levitattention_pa_k_kernel(tc, inputs, w_qkv_words, w_qkv_scales, bn_sc
                 in_=w_qkv_words[group].rearrange("g p n -> p g n").bitcast(I32),
             )
 
-        for s in range(PASSES // SCALE_GROUP):
-            load_w_scales(s)
         load_x(0)
         load_x(1)
         for j in range(CHUNKS):
+            if (j * CHUNK) % SCALE_GROUP == 0:
+                load_w_scales(j * CHUNK // SCALE_GROUP)
             load_w(j)
             if j + 2 < CHUNKS:
                 load_x(j + 2)
@@ -137,27 +138,33 @@ def tile_levitattention_pa_k_kernel(tc, inputs, w_qkv_words, w_qkv_scales, bn_sc
             for ch in range(HALVES):
                 acc[(rt, ch)] = sums.tile([P, HALF], F32, name="acc%d%d" % (rt, ch))
 
-        def multiply(j):
+        def multiply(j, ch):
             x_codes, x_scales = codes_of[j]
-            for ch in range(HALVES):
-                for g in range(CHUNK):
-                    k = j * CHUNK + g
-                    for rt in range(ROW_TILES):
-                        rows = slice(rt * P, (rt + 1) * P)
-                        nc.tensor.matmul_mx(
-                            out=acc[(rt, ch)][:],
-                            lhsT=x_codes[:, g, rows].bitcast(FP8X4),
-                            lhsT_scale=x_scales[:, g, rows],
-                            rhs=w_words[j][:, g, ch * 2 * HALF : (ch + 1) * 2 * HALF].bitcast(FP4X4),
-                            rhs_scale=w_scales[k // SCALE_GROUP][:, k % SCALE_GROUP, ch * HALF : (ch + 1) * HALF],
-                            start=(k == 0),
-                            stop=(k == PASSES - 1),
-                        )
+            for g in range(CHUNK):
+                k = j * CHUNK + g
+                for rt in range(ROW_TILES):
+                    rows = slice(rt * P, (rt + 1) * P)
+                    nc.tensor.matmul_mx(
+                        out=acc[(rt, ch)][:],
+                        lhsT=x_codes[:, g, rows].bitcast(FP8X4),
+                        lhsT_scale=x_scales[:, g, rows],
+                        rhs=w_words[j][:, g, ch * 2 * HALF : (ch + 1) * 2 * HALF].bitcast(FP4X4),
+                        rhs_scale=w_scales[k // SCALE_GROUP][:, k % SCALE_GROUP, ch * HALF : (ch + 1) * HALF],
+                        start=(k == 0),
+                        stop=(k == PASSES - 1),
+                    )
 
         sort_words(0)
-        transpose_and_quantise(0)
         sort_words(1)
+        transpose_and_quantise(0)
+        sort_words(2)
         transpose_and_quantise(1)
+        for j in range(CHUNKS - 2):
+            if j + 3 < CHUNKS:
+                sort_words(j + 3)
+            for ch in range(HALVES):
+                multiply(j, ch)
+            transpose_and_quantise(j + 2)
 
         gain_f32 = const.tile([P, P], F32)
         nc.vector.tensor_copy(out=gain_f32[:], in_=gain_rows[:])
@@ -166,22 +173,20 @@ def tile_levitattention_pa_k_kernel(tc, inputs, w_qkv_words, w_qkv_scales, bn_sc
         gain = const.tile([P, COL_TILES], F32)
         nc.vector.tensor_copy(out=gain[:], in_=gain_bank[:, 0, 0, 0:COL_TILES])
 
-        for j in range(CHUNKS):
-            if j + 2 < CHUNKS:
-                sort_words(j + 2)
-            multiply(j)
-            if j + 2 < CHUNKS:
-                transpose_and_quantise(j + 2)
-
+        copy_of_map = (nc.scalar.copy, nc.vector.tensor_copy)
+        x_rows = {}
         x_cols = {}
         mean_var = {}
         std = {}
         y_cols = {}
+        y_banks = {}
+
+        def sums_to_sbuf(ch):
+            for rt in range(ROW_TILES):
+                x_rows[(rt, ch)] = tail.tile([P, HALF], F32, name="x_rows%d" % rt)
+                copy_of_map[rt](out=x_rows[(rt, ch)][:], in_=acc[(rt, ch)][:])
 
         def column_statistics(ch):
-            x_rows = tail.tile([P, ROW_TILES, HALF], F32)
-            for rt in range(ROW_TILES):
-                nc.scalar.copy(out=x_rows[:, rt, :], in_=acc[(rt, ch)][:])
             stats = tail.tile([P, TILES_PER_HALF, 6], F32)
             mean_var[ch] = tail.tile([P, TILES_PER_HALF, 2], F32, name="mean_var")
             for pair in range(TILES_PER_HALF // 2):
@@ -191,7 +196,7 @@ def tile_levitattention_pa_k_kernel(tc, inputs, w_qkv_words, w_qkv_scales, bn_sc
                     for rt in range(ROW_TILES):
                         nc.tensor.transpose(
                             out=bank[:, i, rt * P : (rt + 1) * P],
-                            in_=x_rows[:, rt, t * P : (t + 1) * P],
+                            in_=x_rows[(rt, ch)][:, t * P : (t + 1) * P],
                             identity=ident[:],
                         )
                     x_cols[(ch, t)] = bank[:, i, :]
@@ -232,17 +237,21 @@ def tile_levitattention_pa_k_kernel(tc, inputs, w_qkv_words, w_qkv_scales, bn_sc
                         bias=shift[:, t : t + 1],
                     )
 
-        def store(ch):
+        def pixels_to_partitions(ch):
             for rt in range(ROW_TILES):
-                y_bank = sums.tile([P, HALF], F32, tag="acc%d%d" % (rt, ch))
+                y_banks[(rt, ch)] = sums.tile([P, HALF], F32, name="y_bank", tag="acc%d%d" % (rt, ch))
                 for t in range(TILES_PER_HALF):
                     nc.tensor.transpose(
-                        out=y_bank[:, t * P : (t + 1) * P],
+                        out=y_banks[(rt, ch)][:, t * P : (t + 1) * P],
                         in_=y_cols[ch][:, t, rt * P : (rt + 1) * P],
                         identity=ident[:],
                     )
+
+        def store(ch):
+            for rt in range(ROW_TILES):
+                y_bank = y_banks[(rt, ch)]
                 y_rows = tail.tile([P, HALF], F32, bufs=ROW_TILES * HALVES)
-                copy_out = nc.scalar.copy if rt == 0 else nc.vector.tensor_copy
+                copy_out = copy_of_map[rt]
                 if ch == 0:
                     copy_out(out=y_rows[:], in_=y_bank[:])
                     for out_dram, first in ((out_0, 0), (out_1, HEADS * DIM)):
@@ -260,11 +269,19 @@ def tile_levitattention_pa_k_kernel(tc, inputs, w_qkv_words, w_qkv_scales, bn_sc
                         in_=y_rows[:].rearrange("n (h e) -> n h e", e=2 * DIM),
                     )
 
-        for ch in range(HALVES):
-            column_statistics(ch)
-        for ch in range(HALVES):
-            standard_deviation(ch)
-        for ch in range(HALVES):
-            normalise(ch)
-        for ch in range(HALVES):
-            store(ch)
+        multiply(CHUNKS - 2, 0)
+        multiply(CHUNKS - 1, 0)
+        sums_to_sbuf(0)
+        multiply(CHUNKS - 2, 1)
+        column_statistics(0)
+        multiply(CHUNKS - 1, 1)
+        standard_deviation(0)
+        normalise(0)
+        sums_to_sbuf(1)
+        pixels_to_partitions(0)
+        column_statistics(1)
+        store(0)
+        standard_deviation(1)
+        normalise(1)
+        pixels_to_partitions(1)
+        store(1)

@@ -23,7 +23,7 @@ HALF = 512
 HALVES = COLS // HALF
 COL_TILES = COLS // P
 TILES_PER_HALF = HALF // P
-CHUNK = 4
+CHUNK = 2
 CHUNKS = PASSES // CHUNK
 SCALE_GROUP = 8
 HEADS = 8

@@ -23,9 +23,9 @@ HALF = 512
 HALVES = COLS // HALF
 COL_TILES = COLS // P
 TILES_PER_HALF = HALF // P
-CHUNK = 2
+CHUNK = 4
 CHUNKS = PASSES // CHUNK
-SCALE_GROUP = 8
+SCALE_GROUP = 4
 HEADS = 8
 DIM = 32
 BN_EPS = 1e-5
@@ -77,12 +77,11 @@ def tile_levitattention_pa_k_kernel(tc, inputs, w_qkv_words, w_qkv_scales, bn_sc
 
         def load_w_scales(s):
             group = slice(s * SCALE_GROUP, (s + 1) * SCALE_GROUP)
-            for b in range(2):
-                for r in range(4):
-                    nc.sync.dma_start(
-                        out=w_scales[s][32 * b + r : P : 64, :, :].bitcast(I32),
-                        in_=w_qkv_scales[group, 4 * b + r : 16 : 8, :].rearrange("g q n -> q g n").bitcast(I32),
-                    )
+            for r in range(4):
+                nc.sync.dma_start(
+                    out=w_scales[s][r : P : 32, :, :].bitcast(I32),
+                    in_=w_qkv_scales[group, r : 16 : 4, :].rearrange("g q n -> q g n").bitcast(I32),
+                )
 
         def load_w(j):
             group = slice(j * CHUNK, (j + 1) * CHUNK)

@@ -23,9 +23,13 @@ HALF = 512
 HALVES = COLS // HALF
 COL_TILES = COLS // P
 TILES_PER_HALF = HALF // P
-CHUNK = 4
-CHUNKS = PASSES // CHUNK
+UNITS = [4] * 8
+FIRST_PASS = [sum(UNITS[:u]) for u in range(len(UNITS))]
+LAST = len(UNITS) - 1
+END = LAST - 1
 SCALE_GROUP = 4
+SCALE_GROUPS = PASSES // SCALE_GROUP
+SCALES_EARLY = 4
 HEADS = 8
 DIM = 32
 BN_EPS = 1e-5
@@ -46,34 +50,35 @@ def tile_levitattention_pa_k_kernel(tc, inputs, w_qkv_words, w_qkv_scales, bn_sc
         sums = ctx.enter_context(tc.psum_pool(name="sums", bufs=1))
         banks = ctx.enter_context(tc.psum_pool(name="banks", bufs=4))
 
-        x_in = resident.tile([P, CHUNKS, ROW_TILES, CHUNK * K_PASS], BF16)
+        x_in = [
+            resident.tile([P, ROW_TILES, n * K_PASS], BF16, name="x_in%d" % u) for u, n in enumerate(UNITS)
+        ]
         w_words = [
-            resident.tile([P, CHUNK, 2 * COLS], U8, name="w_words%d" % j, align_bytes=64) for j in range(CHUNKS)
+            resident.tile([P, n, 2 * COLS], U8, name="w_words%d" % u, align_bytes=64) for u, n in enumerate(UNITS)
         ]
         w_scales = [
             resident.tile([P, SCALE_GROUP, COLS], U8, name="w_scales%d" % s, align_bytes=64)
-            for s in range(PASSES // SCALE_GROUP)
+            for s in range(SCALE_GROUPS)
         ]
 
+        ident = const.tile([P, P], F32)
+        make_identity(nc, ident[:])
         def zero_scale_planes(s):
             nc.vector.memset(w_scales[s][:].bitcast(I32), 0)
 
-        zero_scale_planes(0)
+        for s in range(SCALES_EARLY):
+            zero_scale_planes(s)
         eps = const.tile([P, 1], F32)
         nc.vector.memset(eps[:], BN_EPS)
         gain_rows = const.tile([P, P], BF16)
         nc.vector.memset(gain_rows[:], 0.0)
-        for s in range(1, PASSES // SCALE_GROUP):
-            zero_scale_planes(s)
-        ident = const.tile([P, P], F32)
-        make_identity(nc, ident[:])
         warm = const.tile([P, 1], F32)
-        nc.scalar.activation(out=warm[:], in_=eps[:], func=ACT.Sqrt)
+        nc.scalar.activation(out=warm[:], in_=eps[:], func=ACT.Abs_reciprocal_sqrt)
         nc.scalar.dma_start(out=gain_rows[0:COL_TILES, :], in_=bn_scale.rearrange("(t c) -> t c", c=P))
 
-        def load_x(j):
-            cols = slice(j * CHUNK * K_PASS, (j + 1) * CHUNK * K_PASS)
-            nc.sync.dma_start(out=x_in[:, j], in_=x_dram[:, cols].rearrange("(rt p) k -> p rt k", p=P))
+        def load_x(u):
+            cols = slice(FIRST_PASS[u] * K_PASS, (FIRST_PASS[u] + UNITS[u]) * K_PASS)
+            nc.sync.dma_start(out=x_in[u][:], in_=x_dram[:, cols].rearrange("(rt p) k -> p rt k", p=P))
 
         def load_w_scales(s):
             group = slice(s * SCALE_GROUP, (s + 1) * SCALE_GROUP)
@@ -83,204 +88,277 @@ def tile_levitattention_pa_k_kernel(tc, inputs, w_qkv_words, w_qkv_scales, bn_sc
                     in_=w_qkv_scales[group, r : 16 : 4, :].rearrange("g q n -> q g n").bitcast(I32),
                 )
 
-        def load_w(j):
-            group = slice(j * CHUNK, (j + 1) * CHUNK)
+        def load_w(u):
+            load_w_scales(u)
+            group = slice(FIRST_PASS[u], FIRST_PASS[u] + UNITS[u])
             nc.sync.dma_start(
-                out=w_words[j][:].bitcast(I32),
+                out=w_words[u][:].bitcast(I32),
                 in_=w_qkv_words[group].rearrange("g p n -> p g n").bitcast(I32),
             )
 
+        def load(u):
+            load_w(u)
+            if u + 2 <= LAST:
+                load_x(u + 2)
+
         load_x(0)
         load_x(1)
-        for j in range(CHUNKS):
-            if (j * CHUNK) % SCALE_GROUP == 0:
-                load_w_scales(j * CHUNK // SCALE_GROUP)
-            load_w(j)
-            if j + 2 < CHUNKS:
-                load_x(j + 2)
+        for u in range(SCALES_EARLY):
+            load(u)
 
         sorted_of = {}
         codes_of = {}
 
-        def sort_words(j):
-            x_sorted = stage.tile([P, ROW_TILES, CHUNK, 2, P], F32)
+        def sort_words(u):
+            x_sorted = stage.tile([P, ROW_TILES, UNITS[u], 2, P], F32)
             for rt in range(ROW_TILES):
                 nc.vector.tensor_copy(
                     out=x_sorted[:, rt],
-                    in_=x_in[:, j, rt, :].bitcast(F32).rearrange("r (g q u) -> r g u q", g=CHUNK, u=2),
+                    in_=x_in[u][:, rt, :].bitcast(F32).rearrange("r (g q v) -> r g v q", g=UNITS[u], v=2),
                 )
-            sorted_of[j] = x_sorted
+            sorted_of[u] = x_sorted
 
-        def transpose_and_quantise(j):
-            x_sorted = sorted_of[j]
-            grouped = stage.tile([P, CHUNK, ROW_TILES * P * 4], BF16, align_bytes=64)
-            x_codes = stage.tile([P, CHUNK, ROW_TILES * P], U32, align_bytes=64)
-            x_scales = stage.tile([P, CHUNK, ROW_TILES * P], U8, align_bytes=64)
-            for g in range(CHUNK):
+        def transpose_and_quantise(u):
+            x_sorted = sorted_of[u]
+            grouped = stage.tile([P, UNITS[u], ROW_TILES * P * 4], BF16, align_bytes=64)
+            x_codes = stage.tile([P, UNITS[u], ROW_TILES * P], U32, align_bytes=64, bufs=3)
+            x_scales = stage.tile([P, UNITS[u], ROW_TILES * P], U8, align_bytes=64, bufs=3)
+            for g in range(UNITS[u]):
                 bank = banks.tile([P, ROW_TILES, 2, P], F32, tag="bank")
                 for rt in range(ROW_TILES):
-                    for u in range(2):
-                        nc.tensor.transpose(out=bank[:, rt, u, :], in_=x_sorted[:, rt, g, u, :], identity=ident[:])
+                    for v in range(2):
+                        nc.tensor.transpose(out=bank[:, rt, v, :], in_=x_sorted[:, rt, g, v, :], identity=ident[:])
                 nc.scalar.copy(
-                    out=grouped[:, g, :].bitcast(F32).rearrange("q (rt r u) -> q rt r u", rt=ROW_TILES, u=2),
-                    in_=bank[:].rearrange("q rt u r -> q rt r u"),
+                    out=grouped[:, g, :].bitcast(F32).rearrange("q (rt r v) -> q rt r v", rt=ROW_TILES, v=2),
+                    in_=bank[:].rearrange("q rt v r -> q rt r v"),
                 )
                 nc.vector.quantize_mx(
                     out=x_codes[:, g, :].bitcast(FP8X4),
                     scales=x_scales[:, g, :],
                     in_=grouped[:, g, :],
                 )
-            codes_of[j] = (x_codes, x_scales)
+            codes_of[u] = (x_codes, x_scales)
 
         acc = {}
         for rt in range(ROW_TILES):
             for ch in range(HALVES):
                 acc[(rt, ch)] = sums.tile([P, HALF], F32, name="acc%d%d" % (rt, ch))
 
-        def multiply(j, ch):
-            x_codes, x_scales = codes_of[j]
-            for g in range(CHUNK):
-                k = j * CHUNK + g
+        def last_pass(ch):
+            return (PASSES if ch == 0 else FIRST_PASS[END]) - 1
+
+        def multiply(u, ch):
+            x_codes, x_scales = codes_of[u]
+            for g in range(UNITS[u]):
+                k = FIRST_PASS[u] + g
                 for rt in range(ROW_TILES):
                     rows = slice(rt * P, (rt + 1) * P)
                     nc.tensor.matmul_mx(
                         out=acc[(rt, ch)][:],
                         lhsT=x_codes[:, g, rows].bitcast(FP8X4),
                         lhsT_scale=x_scales[:, g, rows],
-                        rhs=w_words[j][:, g, ch * 2 * HALF : (ch + 1) * 2 * HALF].bitcast(FP4X4),
+                        rhs=w_words[u][:, g, ch * 2 * HALF : (ch + 1) * 2 * HALF].bitcast(FP4X4),
                         rhs_scale=w_scales[k // SCALE_GROUP][:, k % SCALE_GROUP, ch * HALF : (ch + 1) * HALF],
                         start=(k == 0),
-                        stop=(k == PASSES - 1),
+                        stop=(k == last_pass(ch)),
                     )
 
         sort_words(0)
         sort_words(1)
         transpose_and_quantise(0)
+        for s in range(SCALES_EARLY, SCALE_GROUPS):
+            zero_scale_planes(s)
+            load(s)
         sort_words(2)
         transpose_and_quantise(1)
-        for j in range(CHUNKS - 2):
-            if j + 3 < CHUNKS:
-                sort_words(j + 3)
+        for u in range(END):
             for ch in range(HALVES):
-                multiply(j, ch)
-            transpose_and_quantise(j + 2)
+                multiply(u, ch)
+            transpose_and_quantise(u + 2)
+            if u + 3 <= LAST:
+                sort_words(u + 3)
 
-        gain_f32 = const.tile([P, P], F32)
-        nc.vector.tensor_copy(out=gain_f32[:], in_=gain_rows[:])
-        gain_bank = banks.tile([P, ROW_TILES, 2, P], F32, tag="bank")
-        nc.tensor.transpose(out=gain_bank[:, 0, 0, :], in_=gain_f32[:], identity=ident[:])
-        gain = const.tile([P, COL_TILES], F32)
-        nc.vector.tensor_copy(out=gain[:], in_=gain_bank[:, 0, 0, 0:COL_TILES])
+        def load_gain():
+            gain_f32 = const.tile([P, P], F32)
+            nc.vector.tensor_copy(out=gain_f32[:], in_=gain_rows[:])
+            gain_bank = banks.tile([P, ROW_TILES, 2, P], F32, tag="bank")
+            nc.tensor.transpose(out=gain_bank[:, 0, 0, :], in_=gain_f32[:], identity=ident[:])
+            gain_cols = const.tile([P, COL_TILES], F32)
+            nc.vector.tensor_copy(out=gain_cols[:], in_=gain_bank[:, 0, 0, 0:COL_TILES])
+            return gain_cols
 
         copy_of_map = (nc.scalar.copy, nc.vector.tensor_copy)
         x_rows = {}
-        x_cols = {}
-        mean_var = {}
-        std = {}
-        y_cols = {}
-        y_banks = {}
 
         def sums_to_sbuf(ch):
             for rt in range(ROW_TILES):
                 x_rows[(rt, ch)] = tail.tile([P, HALF], F32, name="x_rows%d" % rt)
                 copy_of_map[rt](out=x_rows[(rt, ch)][:], in_=acc[(rt, ch)][:])
 
-        def column_statistics(ch):
-            stats = tail.tile([P, TILES_PER_HALF, 6], F32)
-            mean_var[ch] = tail.tile([P, TILES_PER_HALF, 2], F32, name="mean_var")
-            for pair in range(TILES_PER_HALF // 2):
-                bank = banks.tile([P, 2, ROW_TILES * P], F32, tag="bank")
-                for i in range(2):
-                    t = 2 * pair + i
+        def columns_to_partitions(ch):
+            cols = []
+            for i in range(2):
+                bank = sums.tile([P, 2, ROW_TILES * P], F32, name="x_cols", tag="acc%d%d" % (i, ch))
+                for t in range(2):
                     for rt in range(ROW_TILES):
+                        first = (2 * i + t) * P
                         nc.tensor.transpose(
-                            out=bank[:, i, rt * P : (rt + 1) * P],
-                            in_=x_rows[(rt, ch)][:, t * P : (t + 1) * P],
+                            out=bank[:, t, rt * P : (rt + 1) * P],
+                            in_=x_rows[(rt, ch)][:, first : first + P],
                             identity=ident[:],
                         )
-                    x_cols[(ch, t)] = bank[:, i, :]
-                    nc.vector.bn_stats(out=stats[:, t, :], in_=x_cols[(ch, t)])
-                    nc.vector.bn_aggr(out=mean_var[ch][:, t, :], in_=stats[:, t, :])
+                cols.append(bank)
+            return cols
 
-        def standard_deviation(ch):
-            std[ch] = tail.tile([P, TILES_PER_HALF], F32, name="std")
-            nc.scalar.activation(out=std[ch][:], in_=mean_var[ch][:, :, 1], func=ACT.Sqrt, bias=eps[:])
+        def statistics(x, mean_var):
+            stats = tail.tile([P, 6], F32, bufs=4)
+            nc.vector.bn_stats(out=stats[:], in_=x)
+            nc.vector.bn_aggr(out=mean_var, in_=stats[:])
 
-        def normalise(ch):
-            factor = tail.tile([P, TILES_PER_HALF], F32)
-            shift = tail.tile([P, TILES_PER_HALF], F32)
-            nc.vector.reciprocal(out=factor[:], in_=std[ch][:])
-            nc.vector.tensor_mul(
-                out=factor[:], in0=factor[:], in1=gain[:, ch * TILES_PER_HALF : (ch + 1) * TILES_PER_HALF]
+        def inverse_deviation(name, mean_var, n):
+            rstd = tail.tile([P, n], F32, name=name)
+            nc.scalar.activation(
+                out=rstd[:], in_=mean_var[:, :, 1], func=ACT.Abs_reciprocal_sqrt, bias=eps[:]
             )
-            nc.vector.scalar_tensor_tensor(
-                out=shift[:], in0=mean_var[ch][:, :, 0], scalar=-1.0, in1=factor[:], op0=ALU.mult, op1=ALU.mult
-            )
-            y_cols[ch] = tail.tile([P, TILES_PER_HALF, ROW_TILES * P], F32, name="y_cols")
-            for t in range(TILES_PER_HALF):
-                if t % 2 == 0:
-                    nc.vector.tensor_scalar(
-                        out=y_cols[ch][:, t, :],
-                        in0=x_cols[(ch, t)],
-                        scalar1=factor[:, t : t + 1],
-                        scalar2=shift[:, t : t + 1],
-                        op0=ALU.mult,
-                        op1=ALU.add,
-                    )
-                else:
-                    nc.scalar.activation(
-                        out=y_cols[ch][:, t, :],
-                        in_=x_cols[(ch, t)],
-                        func=ACT.Identity,
-                        scale=factor[:, t : t + 1],
-                        bias=shift[:, t : t + 1],
-                    )
+            return rstd
 
-        def pixels_to_partitions(ch):
+        x_early = tail.tile([P, TILES_PER_HALF, ROW_TILES * P], F32, bufs=1)
+
+        def early_to_columns():
+            for i, bank in enumerate(columns_to_partitions(1)):
+                copy_of_map[i](out=x_early[:, 2 * i : 2 * i + 2, :], in_=bank[:])
+
+        late_of = {}
+
+        def multiply_late(t):
+            late = banks.tile([P, ROW_TILES * P], F32, tag="bank")
+            first = HALF + t * P
             for rt in range(ROW_TILES):
-                y_banks[(rt, ch)] = sums.tile([P, HALF], F32, name="y_bank", tag="acc%d%d" % (rt, ch))
+                rows = slice(rt * P, (rt + 1) * P)
+                for u in range(END, LAST + 1):
+                    x_codes, x_scales = codes_of[u]
+                    for g in range(UNITS[u]):
+                        k = FIRST_PASS[u] + g
+                        nc.tensor.matmul_mx(
+                            out=late[:, rows],
+                            lhsT=w_words[u][:, g, 2 * first : 2 * (first + P)].bitcast(FP4X4),
+                            lhsT_scale=w_scales[k // SCALE_GROUP][:, k % SCALE_GROUP, first : first + P],
+                            rhs=x_codes[:, g, rows].bitcast(FP8X4),
+                            rhs_scale=x_scales[:, g, rows],
+                            start=(k == FIRST_PASS[END]),
+                            stop=(k == PASSES - 1),
+                        )
+            late_of[t] = late
+
+        x_tile = {}
+        mean_var_tile = {}
+        rstd_tile = {}
+        y_tile = {}
+        y_rows_v = [
+            tail.tile([P, ROW_TILES, HEADS // 2, 2, DIM], F32, name="y_rows_v%d" % i, bufs=1) for i in range(2)
+        ]
+
+        def tile_statistics(t):
+            x_tile[t] = tail.tile([P, ROW_TILES * P], F32, name="x_tile")
+            nc.vector.tensor_add(out=x_tile[t][:], in0=late_of[t][:], in1=x_early[:, t, :])
+            mean_var_tile[t] = tail.tile([P, 1, 2], F32, name="mean_var_tile")
+            statistics(x_tile[t][:], mean_var_tile[t][:, 0, :])
+            rstd_tile[t] = inverse_deviation("rstd_tile", mean_var_tile[t], 1)
+
+        def tile_normalise(t):
+            factor = tail.tile([P, 1], F32, name="factor_tile")
+            column = TILES_PER_HALF + t
+            nc.vector.tensor_mul(out=factor[:], in0=rstd_tile[t][:], in1=gain[:, column : column + 1])
+            y_tile[t] = tail.tile([P, ROW_TILES * P], F32, name="y_tile")
+            nc.vector.tensor_scalar(
+                out=y_tile[t][:],
+                in0=x_tile[t][:],
+                scalar1=mean_var_tile[t][:, 0, 0:1],
+                scalar2=factor[:],
+                op0=ALU.subtract,
+                op1=ALU.mult,
+            )
+
+        def tile_to_rows(t):
+            bank = banks.tile([P, ROW_TILES, P], F32, tag="bank")
+            for rt in range(ROW_TILES):
+                nc.tensor.transpose(
+                    out=bank[:, rt, :], in_=y_tile[t][:, rt * P : (rt + 1) * P], identity=ident[:]
+                )
+            nc.scalar.copy(
+                out=y_rows_v[t % 2][:, :, :, t // 2, :], in_=bank[:].rearrange("n rt (h d) -> n rt h d", d=DIM)
+            )
+
+        def store_v(i):
+            for rt in range(ROW_TILES):
+                nc.sync.dma_start(
+                    out=out_2[rt, i * HEADS // 2 : (i + 1) * HEADS // 2].rearrange("h n e -> n h e"),
+                    in_=y_rows_v[i][:, rt].rearrange("n h v d -> n h (v d)"),
+                )
+
+        mean_var_0 = tail.tile([P, TILES_PER_HALF, 2], F32, bufs=1)
+        factor_0 = tail.tile([P, TILES_PER_HALF], F32, bufs=1)
+        shift_0 = tail.tile([P, TILES_PER_HALF], F32, bufs=1)
+        y_cols_0 = tail.tile([P, TILES_PER_HALF, ROW_TILES * P], F32, bufs=1)
+
+        def normalise_0(x_cols, rstd):
+            nc.vector.tensor_mul(out=factor_0[:], in0=rstd[:], in1=gain[:, 0:TILES_PER_HALF])
+            nc.vector.scalar_tensor_tensor(
+                out=shift_0[:], in0=mean_var_0[:, :, 0], scalar=-1.0, in1=factor_0[:], op0=ALU.mult, op1=ALU.mult
+            )
+            for t in range(TILES_PER_HALF):
+                nc.scalar.activation(
+                    out=y_cols_0[:, t, :],
+                    in_=x_cols[t // 2][:, t % 2, :],
+                    func=ACT.Identity,
+                    scale=factor_0[:, t : t + 1],
+                    bias=shift_0[:, t : t + 1],
+                )
+
+        def store_0():
+            for rt in range(ROW_TILES):
+                bank = sums.tile([P, HALF], F32, name="y_bank", tag="acc%d1" % rt)
                 for t in range(TILES_PER_HALF):
                     nc.tensor.transpose(
-                        out=y_banks[(rt, ch)][:, t * P : (t + 1) * P],
-                        in_=y_cols[ch][:, t, rt * P : (rt + 1) * P],
+                        out=bank[:, t * P : (t + 1) * P],
+                        in_=y_cols_0[:, t, rt * P : (rt + 1) * P],
                         identity=ident[:],
                     )
-
-        def store(ch):
-            for rt in range(ROW_TILES):
-                y_bank = y_banks[(rt, ch)]
-                y_rows = tail.tile([P, HALF], F32, bufs=ROW_TILES * HALVES)
-                copy_out = copy_of_map[rt]
-                if ch == 0:
-                    copy_out(out=y_rows[:], in_=y_bank[:])
-                    for out_dram, first in ((out_0, 0), (out_1, HEADS * DIM)):
-                        nc.sync.dma_start(
-                            out=out_dram[rt].rearrange("h n d -> n h d"),
-                            in_=y_rows[:, first : first + HEADS * DIM].rearrange("n (h d) -> n h d", d=DIM),
-                        )
-                else:
-                    copy_out(
-                        out=y_rows[:].rearrange("n (h v d) -> n h v d", v=2, d=DIM),
-                        in_=y_bank[:].rearrange("n (v h d) -> n h v d", v=2, d=DIM),
-                    )
+                y_rows = tail.tile([P, HALF], F32)
+                copy_of_map[rt](out=y_rows[:], in_=bank[:])
+                for out_dram, first in ((out_0, 0), (out_1, HEADS * DIM)):
                     nc.sync.dma_start(
-                        out=out_2[rt].rearrange("h n e -> n h e"),
-                        in_=y_rows[:].rearrange("n (h e) -> n h e", e=2 * DIM),
+                        out=out_dram[rt].rearrange("h n d -> n h d"),
+                        in_=y_rows[:, first : first + HEADS * DIM].rearrange("n (h d) -> n h d", d=DIM),
                     )
 
-        multiply(CHUNKS - 2, 0)
-        multiply(CHUNKS - 1, 0)
-        sums_to_sbuf(0)
-        multiply(CHUNKS - 2, 1)
-        column_statistics(0)
-        multiply(CHUNKS - 1, 1)
-        standard_deviation(0)
-        normalise(0)
         sums_to_sbuf(1)
-        pixels_to_partitions(0)
-        column_statistics(1)
-        store(0)
-        standard_deviation(1)
-        normalise(1)
-        pixels_to_partitions(1)
-        store(1)
+        gain = load_gain()
+        multiply(END, 0)
+        early_to_columns()
+        multiply(LAST, 0)
+        sums_to_sbuf(0)
+        multiply_late(0)
+        x_cols_0 = columns_to_partitions(0)
+        for t in range(TILES_PER_HALF):
+            statistics(x_cols_0[t // 2][:, t % 2, :], mean_var_0[:, t, :])
+        rstd_0 = inverse_deviation("rstd_0", mean_var_0, TILES_PER_HALF)
+        multiply_late(2)
+        tile_statistics(0)
+        normalise_0(x_cols_0, rstd_0)
+        multiply_late(1)
+        tile_normalise(0)
+        tile_statistics(2)
+        store_0()
+        multiply_late(3)
+        tile_normalise(2)
+        tile_statistics(1)
+        tile_to_rows(0)
+        tile_normalise(1)
+        tile_to_rows(2)
+        store_v(0)
+        tile_statistics(3)
+        tile_to_rows(1)
+        tile_normalise(3)
+        tile_to_rows(3)
+        store_v(1)

@@ -23,13 +23,11 @@ HALF = 512
 HALVES = COLS // HALF
 COL_TILES = COLS // P
 TILES_PER_HALF = HALF // P
-UNITS = [4] * 8
-FIRST_PASS = [sum(UNITS[:u]) for u in range(len(UNITS))]
-LAST = len(UNITS) - 1
-END = LAST - 1
-SCALE_GROUP = 4
-SCALE_GROUPS = PASSES // SCALE_GROUP
-SCALES_EARLY = 4
+CHUNK = 4
+CHUNKS = PASSES // CHUNK
+SPLIT = CHUNKS // 2
+LATE = CHUNKS - 2
+ZEROED_FIRST = 3
 HEADS = 8
 DIM = 32
 BN_EPS = 1e-5
@@ -51,23 +49,32 @@ def tile_levitattention_pa_k_kernel(tc, inputs, w_qkv_words, w_qkv_scales, bn_sc
         banks = ctx.enter_context(tc.psum_pool(name="banks", bufs=4))
 
         x_in = [
-            resident.tile([P, ROW_TILES, n * K_PASS], BF16, name="x_in%d" % u) for u, n in enumerate(UNITS)
+            resident.tile([P, ROW_TILES, CHUNK * K_PASS], BF16, name="x_in%d" % j) for j in range(CHUNKS)
         ]
-        w_words = [
-            resident.tile([P, n, 2 * COLS], U8, name="w_words%d" % u, align_bytes=64) for u, n in enumerate(UNITS)
-        ]
+        w_words = {}
+        w_whole = {}
+        for j in range(CHUNKS):
+            if j < SPLIT:
+                whole = resident.tile([P, CHUNK, 2 * COLS], U8, name="w_words%d" % j, align_bytes=64)
+                w_whole[j] = whole
+                for ch in range(HALVES):
+                    w_words[(j, ch)] = whole[:, :, ch * 2 * HALF : (ch + 1) * 2 * HALF]
+            else:
+                for ch in range(HALVES):
+                    half = resident.tile([P, CHUNK, 2 * HALF], U8, name="w_words%d_%d" % (j, ch), align_bytes=64)
+                    w_words[(j, ch)] = half[:]
         w_scales = [
-            resident.tile([P, SCALE_GROUP, COLS], U8, name="w_scales%d" % s, align_bytes=64)
-            for s in range(SCALE_GROUPS)
+            resident.tile([P, CHUNK, COLS], U8, name="w_scales%d" % j, align_bytes=64) for j in range(CHUNKS)
         ]
 
         ident = const.tile([P, P], F32)
         make_identity(nc, ident[:])
-        def zero_scale_planes(s):
-            nc.vector.memset(w_scales[s][:].bitcast(I32), 0)
 
-        for s in range(SCALES_EARLY):
-            zero_scale_planes(s)
+        def zero_scale_planes(j):
+            nc.vector.memset(w_scales[j][:].bitcast(I32), 0)
+
+        for j in range(ZEROED_FIRST):
+            zero_scale_planes(j)
         eps = const.tile([P, 1], F32)
         nc.vector.memset(eps[:], BN_EPS)
         gain_rows = const.tile([P, P], BF16)
@@ -76,54 +83,62 @@ def tile_levitattention_pa_k_kernel(tc, inputs, w_qkv_words, w_qkv_scales, bn_sc
         nc.scalar.activation(out=warm[:], in_=eps[:], func=ACT.Abs_reciprocal_sqrt)
         nc.scalar.dma_start(out=gain_rows[0:COL_TILES, :], in_=bn_scale.rearrange("(t c) -> t c", c=P))
 
-        def load_x(u):
-            cols = slice(FIRST_PASS[u] * K_PASS, (FIRST_PASS[u] + UNITS[u]) * K_PASS)
-            nc.sync.dma_start(out=x_in[u][:], in_=x_dram[:, cols].rearrange("(rt p) k -> p rt k", p=P))
+        def load_x(j):
+            cols = slice(j * CHUNK * K_PASS, (j + 1) * CHUNK * K_PASS)
+            nc.sync.dma_start(out=x_in[j][:], in_=x_dram[:, cols].rearrange("(rt p) k -> p rt k", p=P))
 
-        def load_w_scales(s):
-            group = slice(s * SCALE_GROUP, (s + 1) * SCALE_GROUP)
+        def load_w_scales(j):
+            group = slice(j * CHUNK, (j + 1) * CHUNK)
             for r in range(4):
                 nc.sync.dma_start(
-                    out=w_scales[s][r : P : 32, :, :].bitcast(I32),
+                    out=w_scales[j][r : P : 32, :, :].bitcast(I32),
                     in_=w_qkv_scales[group, r : 16 : 4, :].rearrange("g q n -> q g n").bitcast(I32),
                 )
 
-        def load_w(u):
-            load_w_scales(u)
-            group = slice(FIRST_PASS[u], FIRST_PASS[u] + UNITS[u])
+        def load_w_half(j, ch):
+            group = slice(j * CHUNK, (j + 1) * CHUNK)
+            cols = slice(ch * 2 * HALF, (ch + 1) * 2 * HALF)
             nc.sync.dma_start(
-                out=w_words[u][:].bitcast(I32),
-                in_=w_qkv_words[group].rearrange("g p n -> p g n").bitcast(I32),
+                out=w_words[(j, ch)].bitcast(I32),
+                in_=w_qkv_words[group, :, cols].rearrange("g p n -> p g n").bitcast(I32),
             )
 
-        def load(u):
-            load_w(u)
-            if u + 2 <= LAST:
-                load_x(u + 2)
+        def load(j):
+            load_w_scales(j)
+            if j < SPLIT:
+                group = slice(j * CHUNK, (j + 1) * CHUNK)
+                nc.sync.dma_start(
+                    out=w_whole[j][:].bitcast(I32),
+                    in_=w_qkv_words[group].rearrange("g p n -> p g n").bitcast(I32),
+                )
+            else:
+                load_w_half(j, 0)
+            for next_x in {0: (1,), 1: (2, 3)}.get(j, (j + 2,)):
+                if next_x < CHUNKS:
+                    load_x(next_x)
 
         load_x(0)
-        load_x(1)
-        for u in range(SCALES_EARLY):
-            load(u)
+        for j in range(ZEROED_FIRST):
+            load(j)
 
         sorted_of = {}
         codes_of = {}
 
-        def sort_words(u):
-            x_sorted = stage.tile([P, ROW_TILES, UNITS[u], 2, P], F32)
+        def sort_words(j):
+            x_sorted = stage.tile([P, ROW_TILES, CHUNK, 2, P], F32)
             for rt in range(ROW_TILES):
                 nc.vector.tensor_copy(
                     out=x_sorted[:, rt],
-                    in_=x_in[u][:, rt, :].bitcast(F32).rearrange("r (g q v) -> r g v q", g=UNITS[u], v=2),
+                    in_=x_in[j][:, rt, :].bitcast(F32).rearrange("r (g q v) -> r g v q", g=CHUNK, v=2),
                 )
-            sorted_of[u] = x_sorted
+            sorted_of[j] = x_sorted
 
-        def transpose_and_quantise(u):
-            x_sorted = sorted_of[u]
-            grouped = stage.tile([P, UNITS[u], ROW_TILES * P * 4], BF16, align_bytes=64)
-            x_codes = stage.tile([P, UNITS[u], ROW_TILES * P], U32, align_bytes=64, bufs=3)
-            x_scales = stage.tile([P, UNITS[u], ROW_TILES * P], U8, align_bytes=64, bufs=3)
-            for g in range(UNITS[u]):
+        def transpose_and_quantise(j):
+            x_sorted = sorted_of[j]
+            grouped = stage.tile([P, CHUNK, ROW_TILES * P * 4], BF16, align_bytes=64)
+            x_codes = stage.tile([P, CHUNK, ROW_TILES * P], U32, align_bytes=64, bufs=CHUNKS - SPLIT)
+            x_scales = stage.tile([P, CHUNK, ROW_TILES * P], U8, align_bytes=64, bufs=CHUNKS - SPLIT)
+            for g in range(CHUNK):
                 bank = banks.tile([P, ROW_TILES, 2, P], F32, tag="bank")
                 for rt in range(ROW_TILES):
                     for v in range(2):
@@ -137,46 +152,60 @@ def tile_levitattention_pa_k_kernel(tc, inputs, w_qkv_words, w_qkv_scales, bn_sc
                     scales=x_scales[:, g, :],
                     in_=grouped[:, g, :],
                 )
-            codes_of[u] = (x_codes, x_scales)
+            codes_of[j] = (x_codes, x_scales)
 
         acc = {}
         for rt in range(ROW_TILES):
             for ch in range(HALVES):
                 acc[(rt, ch)] = sums.tile([P, HALF], F32, name="acc%d%d" % (rt, ch))
 
-        def last_pass(ch):
-            return (PASSES if ch == 0 else FIRST_PASS[END]) - 1
+        def matmul_pass(out, k, rt, ch, cols, start, stop):
+            x_codes, x_scales = codes_of[k // CHUNK]
+            g = k % CHUNK
+            rows = slice(rt * P, (rt + 1) * P)
+            nc.tensor.matmul_mx(
+                out=out,
+                lhsT=x_codes[:, g, rows].bitcast(FP8X4),
+                lhsT_scale=x_scales[:, g, rows],
+                rhs=w_words[(k // CHUNK, ch)][:, g, 2 * cols.start : 2 * cols.stop].bitcast(FP4X4),
+                rhs_scale=w_scales[k // CHUNK][:, g, ch * HALF + cols.start : ch * HALF + cols.stop],
+                start=start,
+                stop=stop,
+            )
 
-        def multiply(u, ch):
-            x_codes, x_scales = codes_of[u]
-            for g in range(UNITS[u]):
-                k = FIRST_PASS[u] + g
+        LAST_PASS = (PASSES - 1, LATE * CHUNK - 1)
+
+        def multiply(j, ch):
+            for k in range(j * CHUNK, (j + 1) * CHUNK):
                 for rt in range(ROW_TILES):
-                    rows = slice(rt * P, (rt + 1) * P)
-                    nc.tensor.matmul_mx(
-                        out=acc[(rt, ch)][:],
-                        lhsT=x_codes[:, g, rows].bitcast(FP8X4),
-                        lhsT_scale=x_scales[:, g, rows],
-                        rhs=w_words[u][:, g, ch * 2 * HALF : (ch + 1) * 2 * HALF].bitcast(FP4X4),
-                        rhs_scale=w_scales[k // SCALE_GROUP][:, k % SCALE_GROUP, ch * HALF : (ch + 1) * HALF],
-                        start=(k == 0),
-                        stop=(k == last_pass(ch)),
-                    )
+                    matmul_pass(acc[(rt, ch)][:], k, rt, ch, slice(0, HALF), k == 0, k == LAST_PASS[ch])
 
         sort_words(0)
-        sort_words(1)
         transpose_and_quantise(0)
-        for s in range(SCALES_EARLY, SCALE_GROUPS):
-            zero_scale_planes(s)
-            load(s)
-        sort_words(2)
+        multiply(0, 0)
+        sort_words(1)
         transpose_and_quantise(1)
-        for u in range(END):
-            for ch in range(HALVES):
-                multiply(u, ch)
-            transpose_and_quantise(u + 2)
-            if u + 3 <= LAST:
-                sort_words(u + 3)
+        multiply(0, 1)
+        for j in range(ZEROED_FIRST, CHUNKS):
+            zero_scale_planes(j)
+            load(j)
+            if j == ZEROED_FIRST + 1:
+                sort_words(2)
+        for j in range(SPLIT, CHUNKS):
+            load_w_half(j, 1)
+        multiply(1, 0)
+        transpose_and_quantise(2)
+        multiply(1, 1)
+        sort_words(3)
+        transpose_and_quantise(3)
+        sort_words(4)
+        for j in range(2, CHUNKS):
+            for ch in range(HALVES if j < SPLIT else 1):
+                multiply(j, ch)
+            if j + 2 < CHUNKS:
+                transpose_and_quantise(j + 2)
+            if j + 3 < CHUNKS:
+                sort_words(j + 3)
 
         def load_gain():
             gain_f32 = const.tile([P, P], F32)
@@ -188,27 +217,12 @@ def tile_levitattention_pa_k_kernel(tc, inputs, w_qkv_words, w_qkv_scales, bn_sc
             return gain_cols
 
         copy_of_map = (nc.scalar.copy, nc.vector.tensor_copy)
-        x_rows = {}
 
         def sums_to_sbuf(ch):
+            x_rows = tail.tile([P, ROW_TILES, HALF], F32, name="x_rows%d" % ch, bufs=1)
             for rt in range(ROW_TILES):
-                x_rows[(rt, ch)] = tail.tile([P, HALF], F32, name="x_rows%d" % rt)
-                copy_of_map[rt](out=x_rows[(rt, ch)][:], in_=acc[(rt, ch)][:])
-
-        def columns_to_partitions(ch):
-            cols = []
-            for i in range(2):
-                bank = sums.tile([P, 2, ROW_TILES * P], F32, name="x_cols", tag="acc%d%d" % (i, ch))
-                for t in range(2):
-                    for rt in range(ROW_TILES):
-                        first = (2 * i + t) * P
-                        nc.tensor.transpose(
-                            out=bank[:, t, rt * P : (rt + 1) * P],
-                            in_=x_rows[(rt, ch)][:, first : first + P],
-                            identity=ident[:],
-                        )
-                cols.append(bank)
-            return cols
+                copy_of_map[rt](out=x_rows[:, rt, :], in_=acc[(rt, ch)][:])
+            return x_rows
 
         def statistics(x, mean_var):
             stats = tail.tile([P, 6], F32, bufs=4)
@@ -217,39 +231,62 @@ def tile_levitattention_pa_k_kernel(tc, inputs, w_qkv_words, w_qkv_scales, bn_sc
 
         def inverse_deviation(name, mean_var, n):
             rstd = tail.tile([P, n], F32, name=name)
-            nc.scalar.activation(
-                out=rstd[:], in_=mean_var[:, :, 1], func=ACT.Abs_reciprocal_sqrt, bias=eps[:]
-            )
+            nc.scalar.activation(out=rstd[:], in_=mean_var[:, :, 1], func=ACT.Abs_reciprocal_sqrt, bias=eps[:])
             return rstd
 
-        x_early = tail.tile([P, TILES_PER_HALF, ROW_TILES * P], F32, bufs=1)
+        mean_var_0 = tail.tile([P, TILES_PER_HALF, 2], F32, bufs=1)
+        factor_0 = tail.tile([P, TILES_PER_HALF], F32, bufs=1)
+        shift_0 = tail.tile([P, TILES_PER_HALF], F32, bufs=1)
+        y_cols_0 = tail.tile([P, TILES_PER_HALF, ROW_TILES * P], F32, bufs=1)
 
-        def early_to_columns():
-            for i, bank in enumerate(columns_to_partitions(1)):
-                copy_of_map[i](out=x_early[:, 2 * i : 2 * i + 2, :], in_=bank[:])
+        def columns_0(x_rows):
+            cols = []
+            for pair in range(TILES_PER_HALF // 2):
+                bank = banks.tile([P, 2, ROW_TILES * P], F32, tag="bank")
+                for i in range(2):
+                    t = 2 * pair + i
+                    for rt in range(ROW_TILES):
+                        nc.tensor.transpose(
+                            out=bank[:, i, rt * P : (rt + 1) * P],
+                            in_=x_rows[:, rt, t * P : (t + 1) * P],
+                            identity=ident[:],
+                        )
+                    cols.append(bank[:, i, :])
+                    statistics(cols[t], mean_var_0[:, t, :])
+            return cols
+
+        def normalise_0(x_cols, rstd):
+            nc.vector.tensor_mul(out=factor_0[:], in0=rstd[:], in1=gain[:, 0:TILES_PER_HALF])
+            nc.vector.scalar_tensor_tensor(
+                out=shift_0[:], in0=mean_var_0[:, :, 0], scalar=-1.0, in1=factor_0[:], op0=ALU.mult, op1=ALU.mult
+            )
+            for t in range(TILES_PER_HALF):
+                nc.scalar.activation(
+                    out=y_cols_0[:, t, :],
+                    in_=x_cols[t],
+                    func=ACT.Identity,
+                    scale=factor_0[:, t : t + 1],
+                    bias=shift_0[:, t : t + 1],
+                )
+
+        def store_0():
+            for rt in range(ROW_TILES):
+                bank = sums.tile([P, HALF], F32, name="y_bank", tag="acc%d0" % rt)
+                for t in range(TILES_PER_HALF):
+                    nc.tensor.transpose(
+                        out=bank[:, t * P : (t + 1) * P],
+                        in_=y_cols_0[:, t, rt * P : (rt + 1) * P],
+                        identity=ident[:],
+                    )
+                y_rows = tail.tile([P, HALF], F32)
+                copy_of_map[rt](out=y_rows[:], in_=bank[:])
+                for out_dram, first in ((out_0, 0), (out_1, HEADS * DIM)):
+                    nc.sync.dma_start(
+                        out=out_dram[rt].rearrange("h n d -> n h d"),
+                        in_=y_rows[:, first : first + HEADS * DIM].rearrange("n (h d) -> n h d", d=DIM),
+                    )
 
         late_of = {}
-
-        def multiply_late(t):
-            late = banks.tile([P, ROW_TILES * P], F32, tag="bank")
-            first = HALF + t * P
-            for rt in range(ROW_TILES):
-                rows = slice(rt * P, (rt + 1) * P)
-                for u in range(END, LAST + 1):
-                    x_codes, x_scales = codes_of[u]
-                    for g in range(UNITS[u]):
-                        k = FIRST_PASS[u] + g
-                        nc.tensor.matmul_mx(
-                            out=late[:, rows],
-                            lhsT=w_words[u][:, g, 2 * first : 2 * (first + P)].bitcast(FP4X4),
-                            lhsT_scale=w_scales[k // SCALE_GROUP][:, k % SCALE_GROUP, first : first + P],
-                            rhs=x_codes[:, g, rows].bitcast(FP8X4),
-                            rhs_scale=x_scales[:, g, rows],
-                            start=(k == FIRST_PASS[END]),
-                            stop=(k == PASSES - 1),
-                        )
-            late_of[t] = late
-
         x_tile = {}
         mean_var_tile = {}
         rstd_tile = {}
@@ -258,11 +295,24 @@ def tile_levitattention_pa_k_kernel(tc, inputs, w_qkv_words, w_qkv_scales, bn_sc
             tail.tile([P, ROW_TILES, HEADS // 2, 2, DIM], F32, name="y_rows_v%d" % i, bufs=1) for i in range(2)
         ]
 
-        def tile_statistics(t):
-            x_tile[t] = tail.tile([P, ROW_TILES * P], F32, name="x_tile")
-            nc.vector.tensor_add(out=x_tile[t][:], in0=late_of[t][:], in1=x_early[:, t, :])
+        def multiply_late(t):
+            late = banks.tile([P, ROW_TILES, P], F32, tag="bank")
+            for rt in range(ROW_TILES):
+                for k in range(LATE * CHUNK, PASSES):
+                    matmul_pass(
+                        late[:, rt, :], k, rt, 1, slice(t * P, (t + 1) * P), k == LATE * CHUNK, k == PASSES - 1
+                    )
+            late_of[t] = late
+
+        def tile_statistics(t, x_early):
+            x_rows = tail.tile([P, ROW_TILES, P], F32, name="x_tile_rows")
+            nc.vector.tensor_add(out=x_rows[:], in0=late_of[t][:], in1=x_early[:, :, t * P : (t + 1) * P])
+            bank = banks.tile([P, ROW_TILES * P], F32, tag="bank")
+            for rt in range(ROW_TILES):
+                nc.tensor.transpose(out=bank[:, rt * P : (rt + 1) * P], in_=x_rows[:, rt, :], identity=ident[:])
+            x_tile[t] = bank
             mean_var_tile[t] = tail.tile([P, 1, 2], F32, name="mean_var_tile")
-            statistics(x_tile[t][:], mean_var_tile[t][:, 0, :])
+            statistics(bank[:], mean_var_tile[t][:, 0, :])
             rstd_tile[t] = inverse_deviation("rstd_tile", mean_var_tile[t], 1)
 
         def tile_normalise(t):
@@ -296,68 +346,30 @@ def tile_levitattention_pa_k_kernel(tc, inputs, w_qkv_words, w_qkv_scales, bn_sc
                     in_=y_rows_v[i][:, rt].rearrange("n h v d -> n h (v d)"),
                 )
 
-        mean_var_0 = tail.tile([P, TILES_PER_HALF, 2], F32, bufs=1)
-        factor_0 = tail.tile([P, TILES_PER_HALF], F32, bufs=1)
-        shift_0 = tail.tile([P, TILES_PER_HALF], F32, bufs=1)
-        y_cols_0 = tail.tile([P, TILES_PER_HALF, ROW_TILES * P], F32, bufs=1)
-
-        def normalise_0(x_cols, rstd):
-            nc.vector.tensor_mul(out=factor_0[:], in0=rstd[:], in1=gain[:, 0:TILES_PER_HALF])
-            nc.vector.scalar_tensor_tensor(
-                out=shift_0[:], in0=mean_var_0[:, :, 0], scalar=-1.0, in1=factor_0[:], op0=ALU.mult, op1=ALU.mult
-            )
-            for t in range(TILES_PER_HALF):
-                nc.scalar.activation(
-                    out=y_cols_0[:, t, :],
-                    in_=x_cols[t // 2][:, t % 2, :],
-                    func=ACT.Identity,
-                    scale=factor_0[:, t : t + 1],
-                    bias=shift_0[:, t : t + 1],
-                )
-
-        def store_0():
-            for rt in range(ROW_TILES):
-                bank = sums.tile([P, HALF], F32, name="y_bank", tag="acc%d1" % rt)
-                for t in range(TILES_PER_HALF):
-                    nc.tensor.transpose(
-                        out=bank[:, t * P : (t + 1) * P],
-                        in_=y_cols_0[:, t, rt * P : (rt + 1) * P],
-                        identity=ident[:],
-                    )
-                y_rows = tail.tile([P, HALF], F32)
-                copy_of_map[rt](out=y_rows[:], in_=bank[:])
-                for out_dram, first in ((out_0, 0), (out_1, HEADS * DIM)):
-                    nc.sync.dma_start(
-                        out=out_dram[rt].rearrange("h n d -> n h d"),
-                        in_=y_rows[:, first : first + HEADS * DIM].rearrange("n (h d) -> n h d", d=DIM),
-                    )
-
-        sums_to_sbuf(1)
         gain = load_gain()
-        multiply(END, 0)
-        early_to_columns()
-        multiply(LAST, 0)
-        sums_to_sbuf(0)
-        multiply_late(0)
-        x_cols_0 = columns_to_partitions(0)
-        for t in range(TILES_PER_HALF):
-            statistics(x_cols_0[t // 2][:, t % 2, :], mean_var_0[:, t, :])
+        x_rows_0 = sums_to_sbuf(0)
+        for j in range(SPLIT, LATE - 1):
+            multiply(j, 1)
+        x_cols_0 = columns_0(x_rows_0)
         rstd_0 = inverse_deviation("rstd_0", mean_var_0, TILES_PER_HALF)
-        multiply_late(2)
-        tile_statistics(0)
+        multiply(LATE - 1, 1)
         normalise_0(x_cols_0, rstd_0)
+        x_early_1 = sums_to_sbuf(1)
+        multiply_late(0)
+        store_0()
+        multiply_late(2)
+        tile_statistics(0, x_early_1)
         multiply_late(1)
         tile_normalise(0)
-        tile_statistics(2)
-        store_0()
+        tile_statistics(2, x_early_1)
         multiply_late(3)
-        tile_normalise(2)
-        tile_statistics(1)
         tile_to_rows(0)
-        tile_normalise(1)
+        tile_normalise(2)
+        tile_statistics(1, x_early_1)
         tile_to_rows(2)
         store_v(0)
-        tile_statistics(3)
+        tile_normalise(1)
+        tile_statistics(3, x_early_1)
         tile_to_rows(1)
         tile_normalise(3)
         tile_to_rows(3)

@@ -27,7 +27,7 @@ CHUNK = 4
 CHUNKS = PASSES // CHUNK
 SPLIT = CHUNKS // 2
 LATE = CHUNKS - 2
-ZEROED_FIRST = 3
+SCALE_TILES = 4
 HEADS = 8
 DIM = 32
 BN_EPS = 1e-5
@@ -64,17 +64,14 @@ def tile_levitattention_pa_k_kernel(tc, inputs, w_qkv_words, w_qkv_scales, bn_sc
                     half = resident.tile([P, CHUNK, 2 * HALF], U8, name="w_words%d_%d" % (j, ch), align_bytes=64)
                     w_words[(j, ch)] = half[:]
         w_scales = [
-            resident.tile([P, CHUNK, COLS], U8, name="w_scales%d" % j, align_bytes=64) for j in range(CHUNKS)
+            resident.tile([P, CHUNK, COLS], U8, name="w_scales%d" % i, align_bytes=64) for i in range(SCALE_TILES)
         ]
 
         ident = const.tile([P, P], F32)
         make_identity(nc, ident[:])
-
-        def zero_scale_planes(j):
-            nc.vector.memset(w_scales[j][:].bitcast(I32), 0)
-
-        for j in range(ZEROED_FIRST):
-            zero_scale_planes(j)
+        for i in range(SCALE_TILES):
+            zero = nc.vector.memset if i < SCALE_TILES // 2 else nc.gpsimd.memset
+            zero(w_scales[i][:].bitcast(I32), 0)
         eps = const.tile([P, 1], F32)
         nc.vector.memset(eps[:], BN_EPS)
         gain_rows = const.tile([P, P], BF16)
@@ -91,7 +88,7 @@ def tile_levitattention_pa_k_kernel(tc, inputs, w_qkv_words, w_qkv_scales, bn_sc
             group = slice(j * CHUNK, (j + 1) * CHUNK)
             for r in range(4):
                 nc.sync.dma_start(
-                    out=w_scales[j][r : P : 32, :, :].bitcast(I32),
+                    out=w_scales[j % SCALE_TILES][r : P : 32, :, :].bitcast(I32),
                     in_=w_qkv_scales[group, r : 16 : 4, :].rearrange("g q n -> q g n").bitcast(I32),
                 )
 
@@ -118,7 +115,7 @@ def tile_levitattention_pa_k_kernel(tc, inputs, w_qkv_words, w_qkv_scales, bn_sc
                     load_x(next_x)
 
         load_x(0)
-        for j in range(ZEROED_FIRST):
+        for j in range(SCALE_TILES):
             load(j)
 
         sorted_of = {}
@@ -168,7 +165,7 @@ def tile_levitattention_pa_k_kernel(tc, inputs, w_qkv_words, w_qkv_scales, bn_sc
                 lhsT=x_codes[:, g, rows].bitcast(FP8X4),
                 lhsT_scale=x_scales[:, g, rows],
                 rhs=w_words[(k // CHUNK, ch)][:, g, 2 * cols.start : 2 * cols.stop].bitcast(FP4X4),
-                rhs_scale=w_scales[k // CHUNK][:, g, ch * HALF + cols.start : ch * HALF + cols.stop],
+                rhs_scale=w_scales[k // CHUNK % SCALE_TILES][:, g, ch * HALF + cols.start : ch * HALF + cols.stop],
                 start=start,
                 stop=stop,
             )
@@ -186,26 +183,27 @@ def tile_levitattention_pa_k_kernel(tc, inputs, w_qkv_words, w_qkv_scales, bn_sc
         sort_words(1)
         transpose_and_quantise(1)
         multiply(0, 1)
-        for j in range(ZEROED_FIRST, CHUNKS):
-            zero_scale_planes(j)
-            load(j)
-            if j == ZEROED_FIRST + 1:
-                sort_words(2)
-        for j in range(SPLIT, CHUNKS):
-            load_w_half(j, 1)
+        load(4)
+        sort_words(2)
         multiply(1, 0)
         transpose_and_quantise(2)
         multiply(1, 1)
+        load(5)
         sort_words(3)
         transpose_and_quantise(3)
         sort_words(4)
         for j in range(2, CHUNKS):
             for ch in range(HALVES if j < SPLIT else 1):
                 multiply(j, ch)
+            if j < SPLIT:
+                load(j + SCALE_TILES)
             if j + 2 < CHUNKS:
                 transpose_and_quantise(j + 2)
             if j + 3 < CHUNKS:
                 sort_words(j + 3)
+            if j == SPLIT - 1:
+                for late in range(SPLIT, CHUNKS):
+                    load_w_half(late, 1)
 
         def load_gain():
             gain_f32 = const.tile([P, P], F32)
@@ -252,6 +250,8 @@ def tile_levitattention_pa_k_kernel(tc, inputs, w_qkv_words, w_qkv_scales, bn_sc
                             identity=ident[:],
                         )
                     cols.append(bank[:, i, :])
+                for i in range(2):
+                    t = 2 * pair + i
                     statistics(cols[t], mean_var_0[:, t, :])
             return cols
 
@@ -287,6 +287,7 @@ def tile_levitattention_pa_k_kernel(tc, inputs, w_qkv_words, w_qkv_scales, bn_sc
                     )
 
         late_of = {}
+        x_rows_tile = {}
         x_tile = {}
         mean_var_tile = {}
         rstd_tile = {}
@@ -295,39 +296,51 @@ def tile_levitattention_pa_k_kernel(tc, inputs, w_qkv_words, w_qkv_scales, bn_sc
             tail.tile([P, ROW_TILES, HEADS // 2, 2, DIM], F32, name="y_rows_v%d" % i, bufs=1) for i in range(2)
         ]
 
-        def multiply_late(t):
-            late = banks.tile([P, ROW_TILES, P], F32, tag="bank")
-            for rt in range(ROW_TILES):
-                for k in range(LATE * CHUNK, PASSES):
-                    matmul_pass(
-                        late[:, rt, :], k, rt, 1, slice(t * P, (t + 1) * P), k == LATE * CHUNK, k == PASSES - 1
-                    )
-            late_of[t] = late
+        def multiply_late(t, rt):
+            if rt == 0:
+                late_of[t] = banks.tile([P, ROW_TILES, P], F32, name="late", tag="bank")
+            for k in range(LATE * CHUNK, PASSES):
+                matmul_pass(
+                    late_of[t][:, rt, :], k, rt, 1, slice(t * P, (t + 1) * P), k == LATE * CHUNK, k == PASSES - 1
+                )
 
-        def tile_statistics(t, x_early):
-            x_rows = tail.tile([P, ROW_TILES, P], F32, name="x_tile_rows")
-            nc.vector.tensor_add(out=x_rows[:], in0=late_of[t][:], in1=x_early[:, :, t * P : (t + 1) * P])
-            bank = banks.tile([P, ROW_TILES * P], F32, tag="bank")
+        def tile_add(t, x_early):
+            x_rows_tile[t] = tail.tile([P, ROW_TILES, P], F32, name="x_rows_tile")
+            nc.vector.tensor_add(out=x_rows_tile[t][:], in0=late_of[t][:], in1=x_early[:, :, t * P : (t + 1) * P])
+
+        def tile_statistics(t):
+            x_tile[t] = banks.tile([P, ROW_TILES * P], F32, name="x_tile", tag="bank")
             for rt in range(ROW_TILES):
-                nc.tensor.transpose(out=bank[:, rt * P : (rt + 1) * P], in_=x_rows[:, rt, :], identity=ident[:])
-            x_tile[t] = bank
+                nc.tensor.transpose(
+                    out=x_tile[t][:, rt * P : (rt + 1) * P], in_=x_rows_tile[t][:, rt, :], identity=ident[:]
+                )
             mean_var_tile[t] = tail.tile([P, 1, 2], F32, name="mean_var_tile")
-            statistics(bank[:], mean_var_tile[t][:, 0, :])
+            statistics(x_tile[t][:], mean_var_tile[t][:, 0, :])
             rstd_tile[t] = inverse_deviation("rstd_tile", mean_var_tile[t], 1)
 
-        def tile_normalise(t):
+        def tile_normalise(t, last):
             factor = tail.tile([P, 1], F32, name="factor_tile")
             column = TILES_PER_HALF + t
             nc.vector.tensor_mul(out=factor[:], in0=rstd_tile[t][:], in1=gain[:, column : column + 1])
+            mean = mean_var_tile[t][:, 0, 0:1]
             y_tile[t] = tail.tile([P, ROW_TILES * P], F32, name="y_tile")
-            nc.vector.tensor_scalar(
-                out=y_tile[t][:],
-                in0=x_tile[t][:],
-                scalar1=mean_var_tile[t][:, 0, 0:1],
-                scalar2=factor[:],
-                op0=ALU.subtract,
-                op1=ALU.mult,
-            )
+            if last:
+                nc.vector.tensor_scalar(
+                    out=y_tile[t][:],
+                    in0=x_tile[t][:],
+                    scalar1=mean,
+                    scalar2=factor[:],
+                    op0=ALU.subtract,
+                    op1=ALU.mult,
+                )
+            else:
+                shift = tail.tile([P, 1], F32, name="shift_tile")
+                nc.vector.scalar_tensor_tensor(
+                    out=shift[:], in0=mean, scalar=-1.0, in1=factor[:], op0=ALU.mult, op1=ALU.mult
+                )
+                nc.scalar.activation(
+                    out=y_tile[t][:], in_=x_tile[t][:], func=ACT.Identity, scale=factor[:], bias=shift[:]
+                )
 
         def tile_to_rows(t):
             bank = banks.tile([P, ROW_TILES, P], F32, tag="bank")
@@ -355,22 +368,30 @@ def tile_levitattention_pa_k_kernel(tc, inputs, w_qkv_words, w_qkv_scales, bn_sc
         multiply(LATE - 1, 1)
         normalise_0(x_cols_0, rstd_0)
         x_early_1 = sums_to_sbuf(1)
-        multiply_late(0)
+        multiply_late(0, 0)
+        multiply_late(0, 1)
         store_0()
-        multiply_late(2)
-        tile_statistics(0, x_early_1)
-        multiply_late(1)
-        tile_normalise(0)
-        tile_statistics(2, x_early_1)
-        multiply_late(3)
+        tile_add(0, x_early_1)
+        multiply_late(2, 0)
+        tile_statistics(0)
+        multiply_late(2, 1)
+        tile_add(2, x_early_1)
+        tile_normalise(0, False)
+        multiply_late(1, 0)
+        tile_statistics(2)
+        multiply_late(1, 1)
         tile_to_rows(0)
-        tile_normalise(2)
-        tile_statistics(1, x_early_1)
+        tile_add(1, x_early_1)
+        tile_normalise(2, False)
+        multiply_late(3, 0)
+        tile_statistics(1)
+        multiply_late(3, 1)
         tile_to_rows(2)
         store_v(0)
-        tile_normalise(1)
-        tile_statistics(3, x_early_1)
+        tile_add(3, x_early_1)
+        tile_normalise(1, False)
+        tile_statistics(3)
         tile_to_rows(1)
-        tile_normalise(3)
+        tile_normalise(3, True)
         tile_to_rows(3)
         store_v(1)

@@ -26,8 +26,7 @@ TILES_PER_HALF = HALF // P
 CHUNK = 4
 CHUNKS = PASSES // CHUNK
 SPLIT = CHUNKS // 2
-LATE = CHUNKS - 2
-SCALE_TILES = 4
+LATE = CHUNKS - 1
 HEADS = 8
 DIM = 32
 BN_EPS = 1e-5
@@ -63,15 +62,23 @@ def tile_levitattention_pa_k_kernel(tc, inputs, w_qkv_words, w_qkv_scales, bn_sc
                 for ch in range(HALVES):
                     half = resident.tile([P, CHUNK, 2 * HALF], U8, name="w_words%d_%d" % (j, ch), align_bytes=64)
                     w_words[(j, ch)] = half[:]
-        w_scales = [
-            resident.tile([P, CHUNK, COLS], U8, name="w_scales%d" % i, align_bytes=64) for i in range(SCALE_TILES)
-        ]
+        w_scales = {}
+        s_whole = {}
+        for j in range(CHUNKS):
+            if j < SPLIT:
+                s_whole[j] = resident.tile([P, CHUNK, COLS], U8, name="w_scales%d" % j, align_bytes=64)
+                for ch in range(HALVES):
+                    w_scales[(j, ch)] = s_whole[j][:, :, ch * HALF : (ch + 1) * HALF]
+            else:
+                for ch in range(HALVES):
+                    half = resident.tile([P, CHUNK, HALF], U8, name="w_scales%d_%d" % (j, ch), align_bytes=64)
+                    w_scales[(j, ch)] = half[:]
 
         ident = const.tile([P, P], F32)
         make_identity(nc, ident[:])
-        for i in range(SCALE_TILES):
-            zero = nc.vector.memset if i < SCALE_TILES // 2 else nc.gpsimd.memset
-            zero(w_scales[i][:].bitcast(I32), 0)
+        for j in range(SPLIT):
+            zero = nc.vector.memset if j < SPLIT // 2 else nc.gpsimd.memset
+            zero(s_whole[j][:].bitcast(I32), 0)
         eps = const.tile([P, 1], F32)
         nc.vector.memset(eps[:], BN_EPS)
         gain_rows = const.tile([P, P], BF16)
@@ -84,15 +91,16 @@ def tile_levitattention_pa_k_kernel(tc, inputs, w_qkv_words, w_qkv_scales, bn_sc
             cols = slice(j * CHUNK * K_PASS, (j + 1) * CHUNK * K_PASS)
             nc.sync.dma_start(out=x_in[j][:], in_=x_dram[:, cols].rearrange("(rt p) k -> p rt k", p=P))
 
-        def load_w_scales(j):
+        def load_w_scales(j, cols, planes):
             group = slice(j * CHUNK, (j + 1) * CHUNK)
             for r in range(4):
                 nc.sync.dma_start(
-                    out=w_scales[j % SCALE_TILES][r : P : 32, :, :].bitcast(I32),
-                    in_=w_qkv_scales[group, r : 16 : 4, :].rearrange("g q n -> q g n").bitcast(I32),
+                    out=planes[r : P : 32, :, :].bitcast(I32),
+                    in_=w_qkv_scales[group, r : 16 : 4, cols].rearrange("g q n -> q g n").bitcast(I32),
                 )
 
         def load_w_half(j, ch):
+            load_w_scales(j, slice(ch * HALF, (ch + 1) * HALF), w_scales[(j, ch)])
             group = slice(j * CHUNK, (j + 1) * CHUNK)
             cols = slice(ch * 2 * HALF, (ch + 1) * 2 * HALF)
             nc.sync.dma_start(
@@ -101,21 +109,23 @@ def tile_levitattention_pa_k_kernel(tc, inputs, w_qkv_words, w_qkv_scales, bn_sc
             )
 
         def load(j):
-            load_w_scales(j)
             if j < SPLIT:
+                load_w_scales(j, slice(0, COLS), s_whole[j])
                 group = slice(j * CHUNK, (j + 1) * CHUNK)
                 nc.sync.dma_start(
                     out=w_whole[j][:].bitcast(I32),
                     in_=w_qkv_words[group].rearrange("g p n -> p g n").bitcast(I32),
                 )
             else:
+                for ch in range(HALVES):
+                    nc.vector.memset(w_scales[(j, ch)].bitcast(I32), 0)
                 load_w_half(j, 0)
             for next_x in {0: (1,), 1: (2, 3)}.get(j, (j + 2,)):
                 if next_x < CHUNKS:
                     load_x(next_x)
 
         load_x(0)
-        for j in range(SCALE_TILES):
+        for j in range(SPLIT):
             load(j)
 
         sorted_of = {}
@@ -165,7 +175,7 @@ def tile_levitattention_pa_k_kernel(tc, inputs, w_qkv_words, w_qkv_scales, bn_sc
                 lhsT=x_codes[:, g, rows].bitcast(FP8X4),
                 lhsT_scale=x_scales[:, g, rows],
                 rhs=w_words[(k // CHUNK, ch)][:, g, 2 * cols.start : 2 * cols.stop].bitcast(FP4X4),
-                rhs_scale=w_scales[k // CHUNK % SCALE_TILES][:, g, ch * HALF + cols.start : ch * HALF + cols.stop],
+                rhs_scale=w_scales[(k // CHUNK, ch)][:, g, cols],
                 start=start,
                 stop=stop,
             )
@@ -183,25 +193,25 @@ def tile_levitattention_pa_k_kernel(tc, inputs, w_qkv_words, w_qkv_scales, bn_sc
         sort_words(1)
         transpose_and_quantise(1)
         multiply(0, 1)
-        load(4)
         sort_words(2)
+        load(SPLIT)
         multiply(1, 0)
         transpose_and_quantise(2)
         multiply(1, 1)
-        load(5)
         sort_words(3)
+        load(SPLIT + 1)
         transpose_and_quantise(3)
         sort_words(4)
+        load(SPLIT + 2)
         for j in range(2, CHUNKS):
             for ch in range(HALVES if j < SPLIT else 1):
                 multiply(j, ch)
-            if j < SPLIT:
-                load(j + SCALE_TILES)
             if j + 2 < CHUNKS:
                 transpose_and_quantise(j + 2)
             if j + 3 < CHUNKS:
                 sort_words(j + 3)
-            if j == SPLIT - 1:
+            if j == 2:
+                load(SPLIT + 3)
                 for late in range(SPLIT, CHUNKS):
                     load_w_half(late, 1)
 
@@ -296,13 +306,13 @@ def tile_levitattention_pa_k_kernel(tc, inputs, w_qkv_words, w_qkv_scales, bn_sc
             tail.tile([P, ROW_TILES, HEADS // 2, 2, DIM], F32, name="y_rows_v%d" % i, bufs=1) for i in range(2)
         ]
 
-        def multiply_late(t, rt):
-            if rt == 0:
-                late_of[t] = banks.tile([P, ROW_TILES, P], F32, name="late", tag="bank")
-            for k in range(LATE * CHUNK, PASSES):
-                matmul_pass(
-                    late_of[t][:, rt, :], k, rt, 1, slice(t * P, (t + 1) * P), k == LATE * CHUNK, k == PASSES - 1
-                )
+        def multiply_late(t):
+            late_of[t] = banks.tile([P, ROW_TILES, P], F32, name="late", tag="bank")
+            for rt in range(ROW_TILES):
+                for k in range(LATE * CHUNK, PASSES):
+                    matmul_pass(
+                        late_of[t][:, rt, :], k, rt, 1, slice(t * P, (t + 1) * P), k == LATE * CHUNK, k == PASSES - 1
+                    )
 
         def tile_add(t, x_early):
             x_rows_tile[t] = tail.tile([P, ROW_TILES, P], F32, name="x_rows_tile")
@@ -361,34 +371,30 @@ def tile_levitattention_pa_k_kernel(tc, inputs, w_qkv_words, w_qkv_scales, bn_sc
 
         gain = load_gain()
         x_rows_0 = sums_to_sbuf(0)
-        for j in range(SPLIT, LATE - 1):
-            multiply(j, 1)
+        multiply(SPLIT, 1)
         x_cols_0 = columns_0(x_rows_0)
         rstd_0 = inverse_deviation("rstd_0", mean_var_0, TILES_PER_HALF)
-        multiply(LATE - 1, 1)
         normalise_0(x_cols_0, rstd_0)
+        for j in range(SPLIT + 1, LATE):
+            multiply(j, 1)
         x_early_1 = sums_to_sbuf(1)
-        multiply_late(0, 0)
-        multiply_late(0, 1)
         store_0()
+        multiply_late(0)
+        multiply_late(2)
         tile_add(0, x_early_1)
-        multiply_late(2, 0)
         tile_statistics(0)
-        multiply_late(2, 1)
+        multiply_late(1)
         tile_add(2, x_early_1)
         tile_normalise(0, False)
-        multiply_late(1, 0)
         tile_statistics(2)
-        multiply_late(1, 1)
-        tile_to_rows(0)
+        multiply_late(3)
         tile_add(1, x_early_1)
         tile_normalise(2, False)
-        multiply_late(3, 0)
+        tile_to_rows(0)
         tile_statistics(1)
-        multiply_late(3, 1)
+        tile_add(3, x_early_1)
         tile_to_rows(2)
         store_v(0)
-        tile_add(3, x_early_1)
         tile_normalise(1, False)
         tile_statistics(3)
         tile_to_rows(1)

@@ -227,7 +227,7 @@ def tile_levitattention_pa_k_kernel(tc, inputs, w_qkv_words, w_qkv_scales, bn_sc
         copy_of_map = (nc.scalar.copy, nc.vector.tensor_copy)
 
         def sums_to_sbuf(ch):
-            x_rows = tail.tile([P, ROW_TILES, HALF], F32, name="x_rows%d" % ch, bufs=1)
+            x_rows = tail.tile([P, ROW_TILES, HALF], F32, name="x_rows", bufs=1)
             for rt in range(ROW_TILES):
                 copy_of_map[rt](out=x_rows[:, rt, :], in_=acc[(rt, ch)][:])
             return x_rows
@@ -279,7 +279,9 @@ def tile_levitattention_pa_k_kernel(tc, inputs, w_qkv_words, w_qkv_scales, bn_sc
                     bias=shift_0[:, t : t + 1],
                 )
 
-        def store_0():
+        y_bank_0 = []
+
+        def rows_0():
             for rt in range(ROW_TILES):
                 bank = sums.tile([P, HALF], F32, name="y_bank", tag="acc%d0" % rt)
                 for t in range(TILES_PER_HALF):
@@ -288,78 +290,123 @@ def tile_levitattention_pa_k_kernel(tc, inputs, w_qkv_words, w_qkv_scales, bn_sc
                         in_=y_cols_0[:, t, rt * P : (rt + 1) * P],
                         identity=ident[:],
                     )
-                y_rows = tail.tile([P, HALF], F32)
-                copy_of_map[rt](out=y_rows[:], in_=bank[:])
-                for out_dram, first in ((out_0, 0), (out_1, HEADS * DIM)):
-                    nc.sync.dma_start(
-                        out=out_dram[rt].rearrange("h n d -> n h d"),
-                        in_=y_rows[:, first : first + HEADS * DIM].rearrange("n (h d) -> n h d", d=DIM),
-                    )
+                y_bank_0.append(bank)
+
+        def store_0(rt):
+            y_rows = tail.tile([P, HALF], F32)
+            nc.scalar.copy(out=y_rows[:], in_=y_bank_0[rt][:])
+            for out_dram, first in ((out_0, 0), (out_1, HEADS * DIM)):
+                nc.sync.dma_start(
+                    out=out_dram[rt].rearrange("h n d -> n h d"),
+                    in_=y_rows[:, first : first + HEADS * DIM].rearrange("n (h d) -> n h d", d=DIM),
+                )
 
         late_of = {}
-        x_rows_tile = {}
-        x_tile = {}
-        mean_var_tile = {}
-        rstd_tile = {}
-        y_tile = {}
+        x_rows_pair = {}
+        x_pair = {}
+        mean_var_pair = {}
+        rstd_pair = {}
+        factor_pair = {}
+        shift_pair = {}
+        y_pair = {}
+        y_bank_pair = {}
         y_rows_v = [
             tail.tile([P, ROW_TILES, HEADS // 2, 2, DIM], F32, name="y_rows_v%d" % i, bufs=1) for i in range(2)
         ]
+        for i in range(2):
+            mean_var_pair[i] = tail.tile([P, 2, 2], F32, name="mean_var_pair%d" % i, bufs=1)
 
-        def multiply_late(t):
-            late_of[t] = banks.tile([P, ROW_TILES, P], F32, name="late", tag="bank")
+        def multiply_late(i):
+            late_of[i] = banks.tile([P, ROW_TILES, 2, P], F32, name="late", tag="bank")
             for rt in range(ROW_TILES):
-                for k in range(LATE * CHUNK, PASSES):
-                    matmul_pass(
-                        late_of[t][:, rt, :], k, rt, 1, slice(t * P, (t + 1) * P), k == LATE * CHUNK, k == PASSES - 1
+                for v in range(2):
+                    t = i + 2 * v
+                    for k in range(LATE * CHUNK, PASSES):
+                        matmul_pass(
+                            late_of[i][:, rt, v, :],
+                            k,
+                            rt,
+                            1,
+                            slice(t * P, (t + 1) * P),
+                            k == LATE * CHUNK,
+                            k == PASSES - 1,
+                        )
+
+        def pair_add(i, x_early):
+            x_rows_pair[i] = tail.tile([P, ROW_TILES, 2, P], F32, name="x_rows_pair")
+            nc.vector.tensor_add(
+                out=x_rows_pair[i][:],
+                in0=late_of[i][:],
+                in1=x_early[:].rearrange("n rt (v i c) -> n rt i v c", v=2, i=2)[:, :, i],
+            )
+
+        def pair_columns(i):
+            for v in range(2):
+                if i == 0:
+                    x_pair[(i, v)] = banks.tile([P, ROW_TILES * P], F32, name="x_pair", tag="bank")
+                else:
+                    x_pair[(i, v)] = sums.tile([P, ROW_TILES * P], F32, name="x_pair", tag="acc%d1" % v)
+                for rt in range(ROW_TILES):
+                    nc.tensor.transpose(
+                        out=x_pair[(i, v)][:, rt * P : (rt + 1) * P], in_=x_rows_pair[i][:, rt, v, :], identity=ident[:]
                     )
 
-        def tile_add(t, x_early):
-            x_rows_tile[t] = tail.tile([P, ROW_TILES, P], F32, name="x_rows_tile")
-            nc.vector.tensor_add(out=x_rows_tile[t][:], in0=late_of[t][:], in1=x_early[:, :, t * P : (t + 1) * P])
+        def pair_statistics(i, v):
+            statistics(x_pair[(i, v)][:], mean_var_pair[i][:, v, :])
+            if v == 1:
+                rstd_pair[i] = inverse_deviation("rstd_pair", mean_var_pair[i], 2)
 
-        def tile_statistics(t):
-            x_tile[t] = banks.tile([P, ROW_TILES * P], F32, name="x_tile", tag="bank")
-            for rt in range(ROW_TILES):
-                nc.tensor.transpose(
-                    out=x_tile[t][:, rt * P : (rt + 1) * P], in_=x_rows_tile[t][:, rt, :], identity=ident[:]
-                )
-            mean_var_tile[t] = tail.tile([P, 1, 2], F32, name="mean_var_tile")
-            statistics(x_tile[t][:], mean_var_tile[t][:, 0, :])
-            rstd_tile[t] = inverse_deviation("rstd_tile", mean_var_tile[t], 1)
+        def pair_factors(i):
+            factor_pair[i] = tail.tile([P, 2], F32, name="factor_pair")
+            shift_pair[i] = tail.tile([P, 2], F32, name="shift_pair")
+            nc.vector.tensor_mul(
+                out=factor_pair[i][:],
+                in0=rstd_pair[i][:],
+                in1=gain[:, TILES_PER_HALF:COL_TILES].rearrange("c (v i) -> c i v", i=2)[:, i],
+            )
+            nc.vector.scalar_tensor_tensor(
+                out=shift_pair[i][:],
+                in0=mean_var_pair[i][:, :, 0],
+                scalar=-1.0,
+                in1=factor_pair[i][:],
+                op0=ALU.mult,
+                op1=ALU.mult,
+            )
+            y_pair[i] = tail.tile([P, 2, ROW_TILES * P], F32, name="y_pair")
 
-        def tile_normalise(t, last):
-            factor = tail.tile([P, 1], F32, name="factor_tile")
-            column = TILES_PER_HALF + t
-            nc.vector.tensor_mul(out=factor[:], in0=rstd_tile[t][:], in1=gain[:, column : column + 1])
-            mean = mean_var_tile[t][:, 0, 0:1]
-            y_tile[t] = tail.tile([P, ROW_TILES * P], F32, name="y_tile")
-            if last:
-                nc.vector.tensor_scalar(
-                    out=y_tile[t][:],
-                    in0=x_tile[t][:],
-                    scalar1=mean,
-                    scalar2=factor[:],
-                    op0=ALU.subtract,
-                    op1=ALU.mult,
+        def pair_normalise(i, v, on_scalar):
+            if on_scalar:
+                nc.scalar.activation(
+                    out=y_pair[i][:, v, :],
+                    in_=x_pair[(i, v)][:],
+                    func=ACT.Identity,
+                    scale=factor_pair[i][:, v : v + 1],
+                    bias=shift_pair[i][:, v : v + 1],
                 )
             else:
-                shift = tail.tile([P, 1], F32, name="shift_tile")
-                nc.vector.scalar_tensor_tensor(
-                    out=shift[:], in0=mean, scalar=-1.0, in1=factor[:], op0=ALU.mult, op1=ALU.mult
-                )
-                nc.scalar.activation(
-                    out=y_tile[t][:], in_=x_tile[t][:], func=ACT.Identity, scale=factor[:], bias=shift[:]
+                nc.vector.tensor_scalar(
+                    out=y_pair[i][:, v, :],
+                    in0=x_pair[(i, v)][:],
+                    scalar1=factor_pair[i][:, v : v + 1],
+                    scalar2=shift_pair[i][:, v : v + 1],
+                    op0=ALU.mult,
+                    op1=ALU.add,
                 )
 
-        def tile_to_rows(t):
-            bank = banks.tile([P, ROW_TILES, P], F32, tag="bank")
+        def pair_to_rows(i):
             for rt in range(ROW_TILES):
-                nc.tensor.transpose(
-                    out=bank[:, rt, :], in_=y_tile[t][:, rt * P : (rt + 1) * P], identity=ident[:]
-                )
-            nc.scalar.copy(
-                out=y_rows_v[t % 2][:, :, :, t // 2, :], in_=bank[:].rearrange("n rt (h d) -> n rt h d", d=DIM)
+                y_bank_pair[(i, rt)] = banks.tile([P, 2, P], F32, name="y_bank_pair", tag="bank")
+                for v in range(2):
+                    nc.tensor.transpose(
+                        out=y_bank_pair[(i, rt)][:, v, :],
+                        in_=y_pair[i][:, v, rt * P : (rt + 1) * P],
+                        identity=ident[:],
+                    )
+
+        def copy_v(i, rt, copy_out):
+            copy_out(
+                out=y_rows_v[i][:, rt].rearrange("n h v d -> n v h d"),
+                in_=y_bank_pair[(i, rt)][:].rearrange("n v (h d) -> n v h d", d=DIM),
             )
 
         def store_v(i):
@@ -378,26 +425,30 @@ def tile_levitattention_pa_k_kernel(tc, inputs, w_qkv_words, w_qkv_scales, bn_sc
         for j in range(SPLIT + 1, LATE):
             multiply(j, 1)
         x_early_1 = sums_to_sbuf(1)
-        store_0()
         multiply_late(0)
-        multiply_late(2)
-        tile_add(0, x_early_1)
-        tile_statistics(0)
+        pair_add(0, x_early_1)
         multiply_late(1)
-        tile_add(2, x_early_1)
-        tile_normalise(0, False)
-        tile_statistics(2)
-        multiply_late(3)
-        tile_add(1, x_early_1)
-        tile_normalise(2, False)
-        tile_to_rows(0)
-        tile_statistics(1)
-        tile_add(3, x_early_1)
-        tile_to_rows(2)
+        pair_columns(0)
+        rows_0()
+        store_0(0)
+        pair_add(1, x_early_1)
+        pair_statistics(0, 0)
+        pair_statistics(0, 1)
+        pair_columns(1)
+        pair_statistics(1, 0)
+        pair_factors(0)
+        pair_normalise(0, 0, True)
+        pair_normalise(0, 1, True)
+        store_0(1)
+        pair_to_rows(0)
+        pair_statistics(1, 1)
+        pair_factors(1)
+        pair_normalise(1, 0, True)
+        pair_normalise(1, 1, False)
+        pair_to_rows(1)
+        for rt in range(ROW_TILES):
+            copy_v(0, rt, nc.scalar.copy)
         store_v(0)
-        tile_normalise(1, False)
-        tile_statistics(3)
-        tile_to_rows(1)
-        tile_normalise(3, True)
-        tile_to_rows(3)
+        copy_v(1, 0, nc.scalar.copy)
+        copy_v(1, 1, nc.vector.tensor_copy)
         store_v(1)

from contextlib import ExitStack

import concourse.mybir as mybir
from concourse.masks import make_identity

F32 = mybir.dt.float32
BF16 = mybir.dt.bfloat16
I32 = mybir.dt.int32
U32 = mybir.dt.uint32
U8 = mybir.dt.uint8
FP8X4 = mybir.dt.float8_e4m3fn_x4
FP4X4 = mybir.dt.float4_e2m1fn_x4
ACT = mybir.ActivationFunctionType
ALU = mybir.AluOpType

P = 128
ROW_TILES = 2
CHANNELS = 16384
K_PASS = 512
PASSES = CHANNELS // K_PASS
COLS = 1024
HALF = 512
HALVES = COLS // HALF
COL_TILES = COLS // P
TILES_PER_HALF = HALF // P
CHUNK = 4
CHUNKS = PASSES // CHUNK
SPLIT = CHUNKS // 2
LATE = CHUNKS - 1
HEADS = 8
DIM = 32
BN_EPS = 1e-5

FLOPS = 2 * ROW_TILES * P * CHANNELS * COLS


def tile_levitattention_pa_k_kernel(tc, inputs, w_qkv_words, w_qkv_scales, bn_scale, out_0, out_1, out_2):
    nc = tc.nc
    x_dram = inputs.rearrange("b h w c -> (b h w) c")

    with ExitStack() as ctx:
        ctx.enter_context(tc.manual_schedule())
        const = ctx.enter_context(tc.tile_pool(name="const", bufs=1))
        resident = ctx.enter_context(tc.tile_pool(name="resident", bufs=1))
        stage = ctx.enter_context(tc.tile_pool(name="stage", bufs=2))
        tail = ctx.enter_context(tc.tile_pool(name="tail", bufs=2))
        sums = ctx.enter_context(tc.psum_pool(name="sums", bufs=1))
        banks = ctx.enter_context(tc.psum_pool(name="banks", bufs=4))

        x_in = [
            resident.tile([P, ROW_TILES, CHUNK * K_PASS], BF16, name="x_in%d" % j) for j in range(CHUNKS)
        ]
        w_words = {}
        w_whole = {}
        for j in range(CHUNKS):
            if j < SPLIT:
                whole = resident.tile([P, CHUNK, 2 * COLS], U8, name="w_words%d" % j, align_bytes=64)
                w_whole[j] = whole
                for ch in range(HALVES):
                    w_words[(j, ch)] = whole[:, :, ch * 2 * HALF : (ch + 1) * 2 * HALF]
            else:
                for ch in range(HALVES):
                    half = resident.tile([P, CHUNK, 2 * HALF], U8, name="w_words%d_%d" % (j, ch), align_bytes=64)
                    w_words[(j, ch)] = half[:]
        w_scales = {}
        s_whole = {}
        for j in range(CHUNKS):
            if j < SPLIT:
                s_whole[j] = resident.tile([P, CHUNK, COLS], U8, name="w_scales%d" % j, align_bytes=64)
                for ch in range(HALVES):
                    w_scales[(j, ch)] = s_whole[j][:, :, ch * HALF : (ch + 1) * HALF]
            else:
                for ch in range(HALVES):
                    half = resident.tile([P, CHUNK, HALF], U8, name="w_scales%d_%d" % (j, ch), align_bytes=64)
                    w_scales[(j, ch)] = half[:]

        ident = const.tile([P, P], F32)
        make_identity(nc, ident[:])
        for j in range(SPLIT):
            zero = nc.vector.memset if j < SPLIT // 2 else nc.gpsimd.memset
            zero(s_whole[j][:].bitcast(I32), 0)
        eps = const.tile([P, 1], F32)
        nc.vector.memset(eps[:], BN_EPS)
        gain_rows = const.tile([P, P], BF16)
        nc.vector.memset(gain_rows[:], 0.0)
        warm = const.tile([P, 1], F32)
        nc.scalar.activation(out=warm[:], in_=eps[:], func=ACT.Abs_reciprocal_sqrt)
        nc.scalar.dma_start(out=gain_rows[0:COL_TILES, :], in_=bn_scale.rearrange("(t c) -> t c", c=P))

        def load_x(j):
            cols = slice(j * CHUNK * K_PASS, (j + 1) * CHUNK * K_PASS)
            nc.sync.dma_start(out=x_in[j][:], in_=x_dram[:, cols].rearrange("(rt p) k -> p rt k", p=P))

        def load_w_scales(j, cols, planes):
            group = slice(j * CHUNK, (j + 1) * CHUNK)
            for r in range(4):
                nc.sync.dma_start(
                    out=planes[r : P : 32, :, :].bitcast(I32),
                    in_=w_qkv_scales[group, r : 16 : 4, cols].rearrange("g q n -> q g n").bitcast(I32),
                )

        def load_w_half(j, ch):
            load_w_scales(j, slice(ch * HALF, (ch + 1) * HALF), w_scales[(j, ch)])
            group = slice(j * CHUNK, (j + 1) * CHUNK)
            cols = slice(ch * 2 * HALF, (ch + 1) * 2 * HALF)
            nc.sync.dma_start(
                out=w_words[(j, ch)].bitcast(I32),
                in_=w_qkv_words[group, :, cols].rearrange("g p n -> p g n").bitcast(I32),
            )

        def load(j):
            if j < SPLIT:
                load_w_scales(j, slice(0, COLS), s_whole[j])
                group = slice(j * CHUNK, (j + 1) * CHUNK)
                nc.sync.dma_start(
                    out=w_whole[j][:].bitcast(I32),
                    in_=w_qkv_words[group].rearrange("g p n -> p g n").bitcast(I32),
                )
            else:
                for ch in range(HALVES):
                    nc.vector.memset(w_scales[(j, ch)].bitcast(I32), 0)
                load_w_half(j, 0)
            for next_x in {0: (1,), 1: (2, 3)}.get(j, (j + 2,)):
                if next_x < CHUNKS:
                    load_x(next_x)

        load_x(0)
        for j in range(SPLIT):
            load(j)

        sorted_of = {}
        codes_of = {}

        def sort_words(j):
            x_sorted = stage.tile([P, ROW_TILES, CHUNK, 2, P], F32)
            for rt in range(ROW_TILES):
                nc.vector.tensor_copy(
                    out=x_sorted[:, rt],
                    in_=x_in[j][:, rt, :].bitcast(F32).rearrange("r (g q v) -> r g v q", g=CHUNK, v=2),
                )
            sorted_of[j] = x_sorted

        def transpose_and_quantise(j):
            x_sorted = sorted_of[j]
            grouped = stage.tile([P, CHUNK, ROW_TILES * P * 4], BF16, align_bytes=64)
            x_codes = stage.tile([P, CHUNK, ROW_TILES * P], U32, align_bytes=64, bufs=CHUNKS - SPLIT)
            x_scales = stage.tile([P, CHUNK, ROW_TILES * P], U8, align_bytes=64, bufs=CHUNKS - SPLIT)
            for g in range(CHUNK):
                bank = banks.tile([P, ROW_TILES, 2, P], F32, tag="bank")
                for rt in range(ROW_TILES):
                    for v in range(2):
                        nc.tensor.transpose(out=bank[:, rt, v, :], in_=x_sorted[:, rt, g, v, :], identity=ident[:])
                nc.scalar.copy(
                    out=grouped[:, g, :].bitcast(F32).rearrange("q (rt r v) -> q rt r v", rt=ROW_TILES, v=2),
                    in_=bank[:].rearrange("q rt v r -> q rt r v"),
                )
                nc.vector.quantize_mx(
                    out=x_codes[:, g, :].bitcast(FP8X4),
                    scales=x_scales[:, g, :],
                    in_=grouped[:, g, :],
                )
            codes_of[j] = (x_codes, x_scales)

        acc = {}
        for rt in range(ROW_TILES):
            for ch in range(HALVES):
                acc[(rt, ch)] = sums.tile([P, HALF], F32, name="acc%d%d" % (rt, ch))

        def matmul_pass(out, k, rt, ch, cols, start, stop):
            x_codes, x_scales = codes_of[k // CHUNK]
            g = k % CHUNK
            rows = slice(rt * P, (rt + 1) * P)
            nc.tensor.matmul_mx(
                out=out,
                lhsT=x_codes[:, g, rows].bitcast(FP8X4),
                lhsT_scale=x_scales[:, g, rows],
                rhs=w_words[(k // CHUNK, ch)][:, g, 2 * cols.start : 2 * cols.stop].bitcast(FP4X4),
                rhs_scale=w_scales[(k // CHUNK, ch)][:, g, cols],
                start=start,
                stop=stop,
            )

        LAST_PASS = (PASSES - 1, LATE * CHUNK - 1)

        def multiply(j, ch):
            for k in range(j * CHUNK, (j + 1) * CHUNK):
                for rt in range(ROW_TILES):
                    matmul_pass(acc[(rt, ch)][:], k, rt, ch, slice(0, HALF), k == 0, k == LAST_PASS[ch])

        sort_words(0)
        transpose_and_quantise(0)
        multiply(0, 0)
        sort_words(1)
        transpose_and_quantise(1)
        multiply(0, 1)
        sort_words(2)
        load(SPLIT)
        multiply(1, 0)
        transpose_and_quantise(2)
        multiply(1, 1)
        sort_words(3)
        load(SPLIT + 1)
        transpose_and_quantise(3)
        sort_words(4)
        load(SPLIT + 2)
        for j in range(2, CHUNKS):
            for ch in range(HALVES if j < SPLIT else 1):
                multiply(j, ch)
            if j + 2 < CHUNKS:
                transpose_and_quantise(j + 2)
            if j + 3 < CHUNKS:
                sort_words(j + 3)
            if j == 2:
                load(SPLIT + 3)
                for late in range(SPLIT, CHUNKS):
                    load_w_half(late, 1)

        def load_gain():
            gain_f32 = const.tile([P, P], F32)
            nc.vector.tensor_copy(out=gain_f32[:], in_=gain_rows[:])
            gain_bank = banks.tile([P, ROW_TILES, 2, P], F32, tag="bank")
            nc.tensor.transpose(out=gain_bank[:, 0, 0, :], in_=gain_f32[:], identity=ident[:])
            gain_cols = const.tile([P, COL_TILES], F32)
            nc.vector.tensor_copy(out=gain_cols[:], in_=gain_bank[:, 0, 0, 0:COL_TILES])
            return gain_cols

        copy_of_map = (nc.scalar.copy, nc.vector.tensor_copy)

        def sums_to_sbuf(ch):
            x_rows = tail.tile([P, ROW_TILES, HALF], F32, name="x_rows", bufs=1)
            for rt in range(ROW_TILES):
                copy_of_map[rt](out=x_rows[:, rt, :], in_=acc[(rt, ch)][:])
            return x_rows

        def statistics(x, mean_var):
            stats = tail.tile([P, 6], F32, bufs=4)
            nc.vector.bn_stats(out=stats[:], in_=x)
            nc.vector.bn_aggr(out=mean_var, in_=stats[:])

        def inverse_deviation(name, mean_var, n):
            rstd = tail.tile([P, n], F32, name=name)
            nc.scalar.activation(out=rstd[:], in_=mean_var[:, :, 1], func=ACT.Abs_reciprocal_sqrt, bias=eps[:])
            return rstd

        mean_var_0 = tail.tile([P, TILES_PER_HALF, 2], F32, bufs=1)
        factor_0 = tail.tile([P, TILES_PER_HALF], F32, bufs=1)
        shift_0 = tail.tile([P, TILES_PER_HALF], F32, bufs=1)
        y_cols_0 = tail.tile([P, TILES_PER_HALF, ROW_TILES * P], F32, bufs=1)

        def columns_0(x_rows):
            cols = []
            for pair in range(TILES_PER_HALF // 2):
                bank = banks.tile([P, 2, ROW_TILES * P], F32, tag="bank")
                for i in range(2):
                    t = 2 * pair + i
                    for rt in range(ROW_TILES):
                        nc.tensor.transpose(
                            out=bank[:, i, rt * P : (rt + 1) * P],
                            in_=x_rows[:, rt, t * P : (t + 1) * P],
                            identity=ident[:],
                        )
                    cols.append(bank[:, i, :])
                for i in range(2):
                    t = 2 * pair + i
                    statistics(cols[t], mean_var_0[:, t, :])
            return cols

        def normalise_0(x_cols, rstd):
            nc.vector.tensor_mul(out=factor_0[:], in0=rstd[:], in1=gain[:, 0:TILES_PER_HALF])
            nc.vector.scalar_tensor_tensor(
                out=shift_0[:], in0=mean_var_0[:, :, 0], scalar=-1.0, in1=factor_0[:], op0=ALU.mult, op1=ALU.mult
            )
            for t in range(TILES_PER_HALF):
                nc.scalar.activation(
                    out=y_cols_0[:, t, :],
                    in_=x_cols[t],
                    func=ACT.Identity,
                    scale=factor_0[:, t : t + 1],
                    bias=shift_0[:, t : t + 1],
                )

        y_bank_0 = []

        def rows_0():
            for rt in range(ROW_TILES):
                bank = sums.tile([P, HALF], F32, name="y_bank", tag="acc%d0" % rt)
                for t in range(TILES_PER_HALF):
                    nc.tensor.transpose(
                        out=bank[:, t * P : (t + 1) * P],
                        in_=y_cols_0[:, t, rt * P : (rt + 1) * P],
                        identity=ident[:],
                    )
                y_bank_0.append(bank)

        def store_0(rt):
            y_rows = tail.tile([P, HALF], F32)
            nc.scalar.copy(out=y_rows[:], in_=y_bank_0[rt][:])
            for out_dram, first in ((out_0, 0), (out_1, HEADS * DIM)):
                nc.sync.dma_start(
                    out=out_dram[rt].rearrange("h n d -> n h d"),
                    in_=y_rows[:, first : first + HEADS * DIM].rearrange("n (h d) -> n h d", d=DIM),
                )

        late_of = {}
        x_rows_pair = {}
        x_pair = {}
        mean_var_pair = {}
        rstd_pair = {}
        factor_pair = {}
        shift_pair = {}
        y_pair = {}
        y_bank_pair = {}
        y_rows_v = [
            tail.tile([P, ROW_TILES, HEADS // 2, 2, DIM], F32, name="y_rows_v%d" % i, bufs=1) for i in range(2)
        ]
        for i in range(2):
            mean_var_pair[i] = tail.tile([P, 2, 2], F32, name="mean_var_pair%d" % i, bufs=1)

        def multiply_late(i):
            late_of[i] = banks.tile([P, ROW_TILES, 2, P], F32, name="late", tag="bank")
            for rt in range(ROW_TILES):
                for v in range(2):
                    t = i + 2 * v
                    for k in range(LATE * CHUNK, PASSES):
                        matmul_pass(
                            late_of[i][:, rt, v, :],
                            k,
                            rt,
                            1,
                            slice(t * P, (t + 1) * P),
                            k == LATE * CHUNK,
                            k == PASSES - 1,
                        )

        def pair_add(i, x_early):
            x_rows_pair[i] = tail.tile([P, ROW_TILES, 2, P], F32, name="x_rows_pair")
            nc.vector.tensor_add(
                out=x_rows_pair[i][:],
                in0=late_of[i][:],
                in1=x_early[:].rearrange("n rt (v i c) -> n rt i v c", v=2, i=2)[:, :, i],
            )

        def pair_columns(i):
            for v in range(2):
                if i == 0:
                    x_pair[(i, v)] = banks.tile([P, ROW_TILES * P], F32, name="x_pair", tag="bank")
                else:
                    x_pair[(i, v)] = sums.tile([P, ROW_TILES * P], F32, name="x_pair", tag="acc%d1" % v)
                for rt in range(ROW_TILES):
                    nc.tensor.transpose(
                        out=x_pair[(i, v)][:, rt * P : (rt + 1) * P], in_=x_rows_pair[i][:, rt, v, :], identity=ident[:]
                    )

        def pair_statistics(i, v):
            statistics(x_pair[(i, v)][:], mean_var_pair[i][:, v, :])
            if v == 1:
                rstd_pair[i] = inverse_deviation("rstd_pair", mean_var_pair[i], 2)

        def pair_factors(i):
            factor_pair[i] = tail.tile([P, 2], F32, name="factor_pair")
            shift_pair[i] = tail.tile([P, 2], F32, name="shift_pair")
            nc.vector.tensor_mul(
                out=factor_pair[i][:],
                in0=rstd_pair[i][:],
                in1=gain[:, TILES_PER_HALF:COL_TILES].rearrange("c (v i) -> c i v", i=2)[:, i],
            )
            nc.vector.scalar_tensor_tensor(
                out=shift_pair[i][:],
                in0=mean_var_pair[i][:, :, 0],
                scalar=-1.0,
                in1=factor_pair[i][:],
                op0=ALU.mult,
                op1=ALU.mult,
            )
            y_pair[i] = tail.tile([P, 2, ROW_TILES * P], F32, name="y_pair")

        def pair_normalise(i, v, on_scalar):
            if on_scalar:
                nc.scalar.activation(
                    out=y_pair[i][:, v, :],
                    in_=x_pair[(i, v)][:],
                    func=ACT.Identity,
                    scale=factor_pair[i][:, v : v + 1],
                    bias=shift_pair[i][:, v : v + 1],
                )
            else:
                nc.vector.tensor_scalar(
                    out=y_pair[i][:, v, :],
                    in0=x_pair[(i, v)][:],
                    scalar1=factor_pair[i][:, v : v + 1],
                    scalar2=shift_pair[i][:, v : v + 1],
                    op0=ALU.mult,
                    op1=ALU.add,
                )

        def pair_to_rows(i):
            for rt in range(ROW_TILES):
                y_bank_pair[(i, rt)] = banks.tile([P, 2, P], F32, name="y_bank_pair", tag="bank")
                for v in range(2):
                    nc.tensor.transpose(
                        out=y_bank_pair[(i, rt)][:, v, :],
                        in_=y_pair[i][:, v, rt * P : (rt + 1) * P],
                        identity=ident[:],
                    )

        def copy_v(i, rt, copy_out):
            copy_out(
                out=y_rows_v[i][:, rt].rearrange("n h v d -> n v h d"),
                in_=y_bank_pair[(i, rt)][:].rearrange("n v (h d) -> n v h d", d=DIM),
            )

        def store_v(i):
            for rt in range(ROW_TILES):
                nc.sync.dma_start(
                    out=out_2[rt, i * HEADS // 2 : (i + 1) * HEADS // 2].rearrange("h n e -> n h e"),
                    in_=y_rows_v[i][:, rt].rearrange("n h v d -> n h (v d)"),
                )

        gain = load_gain()
        x_rows_0 = sums_to_sbuf(0)
        multiply(SPLIT, 1)
        x_cols_0 = columns_0(x_rows_0)
        rstd_0 = inverse_deviation("rstd_0", mean_var_0, TILES_PER_HALF)
        normalise_0(x_cols_0, rstd_0)
        for j in range(SPLIT + 1, LATE):
            multiply(j, 1)
        x_early_1 = sums_to_sbuf(1)
        multiply_late(0)
        pair_add(0, x_early_1)
        multiply_late(1)
        pair_columns(0)
        rows_0()
        store_0(0)
        pair_add(1, x_early_1)
        pair_statistics(0, 0)
        pair_statistics(0, 1)
        pair_columns(1)
        pair_statistics(1, 0)
        pair_factors(0)
        pair_normalise(0, 0, True)
        pair_normalise(0, 1, True)
        store_0(1)
        pair_to_rows(0)
        pair_statistics(1, 1)
        pair_factors(1)
        pair_normalise(1, 0, True)
        pair_normalise(1, 1, False)
        pair_to_rows(1)
        for rt in range(ROW_TILES):
            copy_v(0, rt, nc.scalar.copy)
        store_v(0)
        copy_v(1, 0, nc.scalar.copy)
        copy_v(1, 1, nc.vector.tensor_copy)
        store_v(1)
